import numpy as np
import ml_dtypes


def mxq(x, axis, fmt="e4m3"):
    dtype, down = {"e4m3": (ml_dtypes.float8_e4m3fn, 7), "e5m2": (ml_dtypes.float8_e5m2, 14)}[fmt]
    v = np.moveaxis(np.asarray(x, np.float32).astype(ml_dtypes.bfloat16).astype(np.float64), axis, -1)
    blocks = v.reshape(v.shape[:-1] + (-1, 32))
    amax = np.abs(blocks).max(-1, keepdims=True)
    byte = np.maximum(np.where(amax > 0, np.frexp(amax)[1] - 1 + 127, 0) - down, 1)
    scale = np.exp2(byte - 127.0)
    codes = (blocks / scale).astype(np.float32).astype(dtype).astype(np.float64)
    return np.moveaxis((codes * scale).reshape(v.shape), -1, axis)


WIDE = False


def mx_kscale(k):
    if not WIDE:
        return np.ones(k)
    levels = np.array([10, -10, 5, -5, 0])
    a = np.random.permutation(np.resize(levels, k // 512 * 4)).reshape(k // 512, 4)
    idx = np.arange(k)
    return np.exp2(a[idx // 512, idx % 128 // 32])


BF16 = ml_dtypes.bfloat16


def bf(x):
    return np.asarray(x, np.float32).astype(BF16)


def f64(x):
    return np.asarray(x).astype(np.float64)


B, T, HP, WP, NH, D, DFF = 16, 8, 6, 6, 16, 512, 4096
HW = HP * WP


def setup_inputs():
    s = mx_kscale(D)
    c = np.random.standard_normal((B * T, 1 + HW, D)) * 1.5 / np.sqrt(1 + HW)
    c[:, 0, :] *= 5.0
    return {"ctx_s": bf(c * s),
            "x_res": bf(np.random.standard_normal((B, 1 + HW * T, D)) * 1.1),
            "s_out_w": bf(np.random.standard_normal((D, D)) / np.sqrt(D) / s[:, None]),
            "s_out_b": bf(0.1 * np.random.standard_normal(D))}


def reference(ctx_s, x_res, s_out_w, s_out_b):
    res_s = (mxq(f64(ctx_s), 2, "e4m3") @ mxq(f64(s_out_w), 0, "e4m3")) + f64(s_out_b)
    cls_tok = res_s[:, 0, :].reshape(B, T, D).mean(axis=1, keepdims=True)
    res_p = res_s[:, 1:, :].reshape(B, T, HW, D).swapaxes(1, 2).reshape(B, HW * T, D)
    return f64(x_res) + np.concatenate([cls_tok, res_p], axis=1)

@@ -1,0 +1,194 @@
+from contextlib import ExitStack
+
+import concourse.mybir as mybir
+from concourse.masks import make_identity
+
+F32 = mybir.dt.float32
+BF16 = mybir.dt.bfloat16
+U32 = mybir.dt.uint32
+U8 = mybir.dt.uint8
+FP8X4 = mybir.dt.float8_e4m3fn_x4
+ADD = mybir.AluOpType.add
+
+P = 128
+PACK = 4
+SAMPLES = 16
+FRAMES = 8
+PATCHES = 36
+D = 512
+
+RUN = 4
+CHUNK_ROWS = (P // SAMPLES) * RUN
+CHUNK_PATCHES = CHUNK_ROWS // FRAMES
+CHUNKS = PATCHES // CHUNK_PATCHES
+FRAME_GROUPS = FRAMES // RUN
+
+GPSIMD_TILES = 3
+
+FLOPS = 2 * SAMPLES * FRAMES * (1 + PATCHES) * D * D
+
+
+def transpose_words(nc, flipped, rows, permutation):
+    words = rows.bitcast(F32)
+    for u in range(2):
+        nc.tensor.transpose(flipped[:, u, :], words[:, u * P : (u + 1) * P], permutation)
+
+
+def tile_timesformerlayer_pc_t_kernel(tc, ctx_s, x_res, s_out_w, s_out_b, out):
+    nc = tc.nc
+    with ExitStack() as pools:
+        const = pools.enter_context(tc.tile_pool(name="const", bufs=1))
+        resident = pools.enter_context(tc.tile_pool(name="resident", bufs=1))
+        work = pools.enter_context(tc.tile_pool(name="work", bufs=3))
+        psum_bias = pools.enter_context(tc.psum_pool(name="psum_bias", bufs=1))
+        psum_flip = pools.enter_context(tc.psum_pool(name="psum_flip", bufs=3))
+        psum_prod = pools.enter_context(tc.psum_pool(name="psum_prod", bufs=4))
+
+        w_rows = const.tile([P, PACK, D], BF16)
+        nc.sync.dma_start(
+            out=w_rows[:].rearrange("q (u e) c -> q u (e c)", u=2),
+            in_=s_out_w.rearrange("(u q e) c -> q u (e c)", u=2, e=2),
+        )
+        cls_ctx = resident.tile([P, D], BF16)
+        nc.sync.dma_start(out=cls_ctx[:], in_=ctx_s[:, 0, :])
+        bias_row = const.tile([P, D], BF16)
+        nc.vector.memset(bias_row[:], 0.0)
+        nc.sync.dma_start(out=bias_row[0:1, :], in_=s_out_b.rearrange("(o d) -> o d", o=1))
+        cls_x = resident.tile([SAMPLES, D], BF16)
+        nc.sync.dma_start(out=cls_x[:], in_=x_res[:, 0, :])
+        ctx_chunks = []
+        x_chunks = []
+        for c in range(CHUNKS):
+            ctx_chunk = resident.tile([P, CHUNK_PATCHES, D], BF16, name="ctx_chunk%d" % c)
+            first_patch = 1 + c * CHUNK_PATCHES
+            nc.sync.dma_start(
+                out=ctx_chunk[:], in_=ctx_s[:, first_patch : first_patch + CHUNK_PATCHES, :]
+            )
+            ctx_chunks.append(ctx_chunk)
+            x_chunk = resident.tile([P, RUN, D], BF16, name="x_chunk%d" % c)
+            first_row = 1 + c * CHUNK_ROWS
+            nc.sync.dma_start(
+                out=x_chunk[:].rearrange("p j d -> p (j d)"),
+                in_=x_res[:, first_row : first_row + CHUNK_ROWS, :].rearrange(
+                    "b (x j) d -> b x (j d)", j=RUN
+                ),
+            )
+            x_chunks.append(x_chunk)
+
+        ident = const.tile([P, P], F32)
+        make_identity(nc, ident[:])
+        by_row = const.tile([P, P], F32)
+        nc.vector.tensor_copy(
+            out=by_row[:].rearrange("n (j g) -> n j g", j=RUN),
+            in_=ident[:].rearrange("n (g j) -> n j g", j=RUN),
+        )
+        frame_mean = const.tile([P, P], F32)
+        nc.vector.memset(frame_mean[:], 0.0)
+        nc.vector.tensor_reduce(
+            out=frame_mean[:, 0:SAMPLES],
+            in_=ident[:].rearrange("n (b t) -> n b t", t=FRAMES),
+            axis=mybir.AxisListType.X,
+            op=ADD,
+        )
+        nc.vector.tensor_scalar_mul(
+            out=frame_mean[:, 0:SAMPLES], in0=frame_mean[:, 0:SAMPLES], scalar1=1.0 / FRAMES
+        )
+        ones = const.tile([P, P], BF16)
+        nc.vector.memset(ones[:], 1.0)
+        bias_psum = psum_bias.tile([P, D], F32)
+        nc.tensor.matmul(out=bias_psum[:], lhsT=ones[:], rhs=bias_row[:], start=True, stop=True)
+        bias_sbuf = const.tile([P, D], F32)
+        nc.scalar.copy(out=bias_sbuf[:], in_=bias_psum[:])
+
+        w_grouped = const.tile([P, D, PACK], BF16, align_bytes=64)
+        nc.vector.tensor_copy(out=w_grouped[:], in_=w_rows[:].rearrange("q v c -> q c v"))
+        w_codes = const.tile([P, D], U32, align_bytes=64)
+        w_scales = const.tile([P, D], U8, align_bytes=64)
+        nc.vector.quantize_mx(
+            out=w_codes[:].bitcast(FP8X4),
+            scales=w_scales[:],
+            in_=w_grouped[:].rearrange("q c v -> q (c v)"),
+        )
+
+        def product(codes, scales):
+            prod = psum_prod.tile([P, D], F32, tag="prod")
+            nc.tensor.matmul_mx(
+                out=prod[:],
+                lhsT=codes.bitcast(FP8X4),
+                lhsT_scale=scales,
+                rhs=w_codes[:].bitcast(FP8X4),
+                rhs_scale=w_scales[:],
+                start=True,
+                stop=True,
+            )
+            return prod
+
+        cls_flipped = psum_flip.tile([P, 2, P], F32, tag="flipped")
+        transpose_words(nc, cls_flipped, cls_ctx[:], ident[:])
+        cls_grouped = const.tile([P, P, PACK], BF16, align_bytes=64)
+        nc.scalar.copy(
+            out=cls_grouped[:].bitcast(F32), in_=cls_flipped[:].rearrange("q u n -> q n u")
+        )
+        cls_codes = const.tile([P, P], U32, align_bytes=64)
+        cls_scales = const.tile([P, P], U8, align_bytes=64)
+        nc.vector.quantize_mx(
+            out=cls_codes[:].bitcast(FP8X4),
+            scales=cls_scales[:],
+            in_=cls_grouped[:].rearrange("q n v -> q (n v)"),
+        )
+        cls_prod = product(cls_codes[:], cls_scales[:])
+        cls_res = const.tile([P, D], F32)
+        nc.scalar.copy(out=cls_res[:], in_=cls_prod[:])
+        cls_mean = psum_prod.tile([P, D], F32, tag="prod")
+        nc.tensor.matmul(out=cls_mean[:], lhsT=frame_mean[:], rhs=cls_res[:], start=True, stop=True)
+        cls_out = const.tile([SAMPLES, D], F32)
+        nc.vector.tensor_tensor(out=cls_out[:], in0=cls_x[:], in1=bias_psum[0:SAMPLES, :], op=ADD)
+        nc.vector.tensor_tensor(out=cls_out[:], in0=cls_mean[0:SAMPLES, :], in1=cls_out[:], op=ADD)
+        nc.sync.dma_start(out=out[:, 0, :], in_=cls_out[:])
+
+        for c in range(CHUNKS):
+            out_chunk = resident.tile([P, RUN, D], F32, name="out_chunk%d" % c)
+            nc.gpsimd.tensor_tensor(
+                out=out_chunk[:, 0:GPSIMD_TILES, :],
+                in0=x_chunks[c][:, 0:GPSIMD_TILES, :],
+                in1=bias_sbuf[:].unsqueeze(1).to_broadcast([P, GPSIMD_TILES, D]),
+                op=ADD,
+            )
+            for j in range(GPSIMD_TILES, RUN):
+                nc.vector.tensor_tensor(
+                    out=out_chunk[:, j, :], in0=x_chunks[c][:, j, :], in1=bias_psum[:], op=ADD
+                )
+
+            grouped = work.tile(
+                [P, RUN * SAMPLES, CHUNK_PATCHES, FRAME_GROUPS, PACK], BF16, align_bytes=64
+            )
+            grouped_words = grouped[:].bitcast(F32)
+            for pair in range(CHUNK_PATCHES // 2):
+                flipped = psum_flip.tile([P, 2, 2, P], F32, tag="flipped")
+                for i in range(2):
+                    a = 2 * pair + i
+                    transpose_words(nc, flipped[:, i], ctx_chunks[c][:, a, :], by_row[:])
+                    nc.scalar.copy(
+                        out=grouped_words[:, :, a, :, :],
+                        in_=flipped[:, i].rearrange("q u (m h) -> q m h u", h=FRAME_GROUPS),
+                    )
+            codes = work.tile([P, RUN * P], U32, align_bytes=64)
+            scales = work.tile([P, RUN * P], U8, align_bytes=64)
+            nc.vector.quantize_mx(
+                out=codes[:].bitcast(FP8X4),
+                scales=scales[:],
+                in_=grouped[:].rearrange("q m a h v -> q (m a h v)"),
+            )
+            for j in range(RUN):
+                tokens = slice(j * P, (j + 1) * P)
+                prod = product(codes[:, tokens], scales[:, tokens])
+                nc.vector.tensor_tensor(
+                    out=out_chunk[:, j, :], in0=prod[:], in1=out_chunk[:, j, :], op=ADD
+                )
+            first_row = 1 + c * CHUNK_ROWS
+            nc.sync.dma_start(
+                out=out[:, first_row : first_row + CHUNK_ROWS, :].rearrange(
+                    "b (x j) d -> b x (j d)", j=RUN
+                ),
+                in_=out_chunk[:].rearrange("p j d -> p (j d)"),
+            )

@@ -23,8 +23,6 @@ CHUNK_PATCHES = CHUNK_ROWS // FRAMES
 CHUNKS = PATCHES // CHUNK_PATCHES
 FRAME_GROUPS = FRAMES // RUN
 
-GPSIMD_TILES = 3
-
 FLOPS = 2 * SAMPLES * FRAMES * (1 + PATCHES) * D * D
 
 
@@ -97,8 +95,6 @@ def tile_timesformerlayer_pc_t_kernel(tc, ctx_s, x_res, s_out_w, s_out_b, out):
         nc.vector.memset(ones[:], 1.0)
         bias_psum = psum_bias.tile([P, D], F32)
         nc.tensor.matmul(out=bias_psum[:], lhsT=ones[:], rhs=bias_row[:], start=True, stop=True)
-        bias_sbuf = const.tile([P, D], F32)
-        nc.scalar.copy(out=bias_sbuf[:], in_=bias_psum[:])
 
         w_grouped = const.tile([P, D, PACK], BF16, align_bytes=64)
         nc.vector.tensor_copy(out=w_grouped[:], in_=w_rows[:].rearrange("q v c -> q c v"))
@@ -148,13 +144,7 @@ def tile_timesformerlayer_pc_t_kernel(tc, ctx_s, x_res, s_out_w, s_out_b, out):
 
         for c in range(CHUNKS):
             out_chunk = resident.tile([P, RUN, D], F32, name="out_chunk%d" % c)
-            nc.gpsimd.tensor_tensor(
-                out=out_chunk[:, 0:GPSIMD_TILES, :],
-                in0=x_chunks[c][:, 0:GPSIMD_TILES, :],
-                in1=bias_sbuf[:].unsqueeze(1).to_broadcast([P, GPSIMD_TILES, D]),
-                op=ADD,
-            )
-            for j in range(GPSIMD_TILES, RUN):
+            for j in range(RUN):
                 nc.vector.tensor_tensor(
                     out=out_chunk[:, j, :], in0=x_chunks[c][:, j, :], in1=bias_psum[:], op=ADD
                 )

@@ -9,6 +9,7 @@ U32 = mybir.dt.uint32
 U8 = mybir.dt.uint8
 FP8X4 = mybir.dt.float8_e4m3fn_x4
 ADD = mybir.AluOpType.add
+IDENTITY = mybir.ActivationFunctionType.Identity
 
 P = 128
 PACK = 4
@@ -16,10 +17,12 @@ SAMPLES = 16
 FRAMES = 8
 PATCHES = 36
 D = 512
+D_TILES = D // P
 
 RUN = 4
 CHUNK_ROWS = (P // SAMPLES) * RUN
 CHUNK_PATCHES = CHUNK_ROWS // FRAMES
+CHUNK_TOKENS = RUN * P
 CHUNKS = PATCHES // CHUNK_PATCHES
 FRAME_GROUPS = FRAMES // RUN
 
@@ -34,14 +37,20 @@ def transpose_words(nc, flipped, rows, permutation):
 
 def tile_timesformerlayer_pc_t_kernel(tc, ctx_s, x_res, s_out_w, s_out_b, out):
     nc = tc.nc
-    with ExitStack() as pools:
-        const = pools.enter_context(tc.tile_pool(name="const", bufs=1))
-        resident = pools.enter_context(tc.tile_pool(name="resident", bufs=1))
-        work = pools.enter_context(tc.tile_pool(name="work", bufs=3))
-        psum_bias = pools.enter_context(tc.psum_pool(name="psum_bias", bufs=1))
-        psum_flip = pools.enter_context(tc.psum_pool(name="psum_flip", bufs=3))
-        psum_prod = pools.enter_context(tc.psum_pool(name="psum_prod", bufs=4))
+    with ExitStack() as scope:
+        const = scope.enter_context(tc.tile_pool(name="const", bufs=1))
+        resident = scope.enter_context(tc.tile_pool(name="resident", bufs=1))
+        work = scope.enter_context(tc.tile_pool(name="work", bufs=3))
+        psum_flip = scope.enter_context(tc.psum_pool(name="psum_flip", bufs=2))
+        psum_prod = scope.enter_context(tc.psum_pool(name="psum_prod", bufs=3))
+        psum_back = scope.enter_context(tc.psum_pool(name="psum_back", bufs=3))
+        scope.enter_context(tc.manual_schedule())
 
+        bias_rows = const.tile([P, P], BF16)
+        nc.vector.memset(bias_rows[:], 0.0)
+        nc.sync.dma_start(
+            out=bias_rows[0:D_TILES, :], in_=s_out_b.rearrange("(m d) -> m d", m=D_TILES)
+        )
         w_rows = const.tile([P, PACK, D], BF16)
         nc.sync.dma_start(
             out=w_rows[:].rearrange("q (u e) c -> q u (e c)", u=2),
@@ -49,20 +58,12 @@ def tile_timesformerlayer_pc_t_kernel(tc, ctx_s, x_res, s_out_w, s_out_b, out):
         )
         cls_ctx = resident.tile([P, D], BF16)
         nc.sync.dma_start(out=cls_ctx[:], in_=ctx_s[:, 0, :])
-        bias_row = const.tile([P, D], BF16)
-        nc.vector.memset(bias_row[:], 0.0)
-        nc.sync.dma_start(out=bias_row[0:1, :], in_=s_out_b.rearrange("(o d) -> o d", o=1))
         cls_x = resident.tile([SAMPLES, D], BF16)
         nc.sync.dma_start(out=cls_x[:], in_=x_res[:, 0, :])
         ctx_chunks = []
         x_chunks = []
-        for c in range(CHUNKS):
-            ctx_chunk = resident.tile([P, CHUNK_PATCHES, D], BF16, name="ctx_chunk%d" % c)
-            first_patch = 1 + c * CHUNK_PATCHES
-            nc.sync.dma_start(
-                out=ctx_chunk[:], in_=ctx_s[:, first_patch : first_patch + CHUNK_PATCHES, :]
-            )
-            ctx_chunks.append(ctx_chunk)
+
+        def load_x(c):
             x_chunk = resident.tile([P, RUN, D], BF16, name="x_chunk%d" % c)
             first_row = 1 + c * CHUNK_ROWS
             nc.sync.dma_start(
@@ -73,28 +74,30 @@ def tile_timesformerlayer_pc_t_kernel(tc, ctx_s, x_res, s_out_w, s_out_b, out):
             )
             x_chunks.append(x_chunk)
 
+        for c in range(CHUNKS):
+            ctx_chunk = resident.tile([P, CHUNK_PATCHES, D], BF16, name="ctx_chunk%d" % c)
+            first_patch = 1 + c * CHUNK_PATCHES
+            nc.sync.dma_start(
+                out=ctx_chunk[:], in_=ctx_s[:, first_patch : first_patch + CHUNK_PATCHES, :]
+            )
+            ctx_chunks.append(ctx_chunk)
+            if c >= 1:
+                load_x(c - 1)
+        load_x(CHUNKS - 1)
+
         ident = const.tile([P, P], F32)
         make_identity(nc, ident[:])
+        ident_bf16 = const.tile([P, P], BF16)
+        nc.vector.tensor_copy(out=ident_bf16[:], in_=ident[:])
         by_row = const.tile([P, P], F32)
         nc.vector.tensor_copy(
             out=by_row[:].rearrange("n (j g) -> n j g", j=RUN),
             in_=ident[:].rearrange("n (g j) -> n j g", j=RUN),
         )
-        frame_mean = const.tile([P, P], F32)
-        nc.vector.memset(frame_mean[:], 0.0)
-        nc.vector.tensor_reduce(
-            out=frame_mean[:, 0:SAMPLES],
-            in_=ident[:].rearrange("n (b t) -> n b t", t=FRAMES),
-            axis=mybir.AxisListType.X,
-            op=ADD,
-        )
-        nc.vector.tensor_scalar_mul(
-            out=frame_mean[:, 0:SAMPLES], in0=frame_mean[:, 0:SAMPLES], scalar1=1.0 / FRAMES
-        )
-        ones = const.tile([P, P], BF16)
-        nc.vector.memset(ones[:], 1.0)
-        bias_psum = psum_bias.tile([P, D], F32)
-        nc.tensor.matmul(out=bias_psum[:], lhsT=ones[:], rhs=bias_row[:], start=True, stop=True)
+        bias_flipped = psum_back.tile([P, P], BF16, tag="back")
+        nc.tensor.transpose(bias_flipped[:], bias_rows[:], ident_bf16[:])
+        bias_col = const.tile([P, D_TILES], F32)
+        nc.scalar.copy(out=bias_col[:], in_=bias_flipped[:, 0:D_TILES])
 
         w_grouped = const.tile([P, D, PACK], BF16, align_bytes=64)
         nc.vector.tensor_copy(out=w_grouped[:], in_=w_rows[:].rearrange("q v c -> q c v"))
@@ -106,49 +109,70 @@ def tile_timesformerlayer_pc_t_kernel(tc, ctx_s, x_res, s_out_w, s_out_b, out):
             in_=w_grouped[:].rearrange("q c v -> q (c v)"),
         )
 
-        def product(codes, scales):
-            prod = psum_prod.tile([P, D], F32, tag="prod")
+        def multiply_by_w(prod, m, codes, scales):
+            columns = slice(m * P, (m + 1) * P)
             nc.tensor.matmul_mx(
-                out=prod[:],
-                lhsT=codes.bitcast(FP8X4),
-                lhsT_scale=scales,
-                rhs=w_codes[:].bitcast(FP8X4),
-                rhs_scale=w_scales[:],
+                out=prod,
+                lhsT=w_codes[:, columns].bitcast(FP8X4),
+                lhsT_scale=w_scales[:, columns],
+                rhs=codes.bitcast(FP8X4),
+                rhs_scale=scales,
                 start=True,
                 stop=True,
             )
-            return prod
 
-        cls_flipped = psum_flip.tile([P, 2, P], F32, tag="flipped")
-        transpose_words(nc, cls_flipped, cls_ctx[:], ident[:])
-        cls_grouped = const.tile([P, P, PACK], BF16, align_bytes=64)
-        nc.scalar.copy(
-            out=cls_grouped[:].bitcast(F32), in_=cls_flipped[:].rearrange("q u n -> q n u")
-        )
         cls_codes = const.tile([P, P], U32, align_bytes=64)
         cls_scales = const.tile([P, P], U8, align_bytes=64)
-        nc.vector.quantize_mx(
-            out=cls_codes[:].bitcast(FP8X4),
-            scales=cls_scales[:],
-            in_=cls_grouped[:].rearrange("q n v -> q (n v)"),
-        )
-        cls_prod = product(cls_codes[:], cls_scales[:])
-        cls_res = const.tile([P, D], F32)
-        nc.scalar.copy(out=cls_res[:], in_=cls_prod[:])
-        cls_mean = psum_prod.tile([P, D], F32, tag="prod")
-        nc.tensor.matmul(out=cls_mean[:], lhsT=frame_mean[:], rhs=cls_res[:], start=True, stop=True)
-        cls_out = const.tile([SAMPLES, D], F32)
-        nc.vector.tensor_tensor(out=cls_out[:], in0=cls_x[:], in1=bias_psum[0:SAMPLES, :], op=ADD)
-        nc.vector.tensor_tensor(out=cls_out[:], in0=cls_mean[0:SAMPLES, :], in1=cls_out[:], op=ADD)
-        nc.sync.dma_start(out=out[:, 0, :], in_=cls_out[:])
+        cls_mean = const.tile([P, D_TILES, P], F32)
+        nc.vector.memset(cls_mean[:], 0.0)
 
-        for c in range(CHUNKS):
-            out_chunk = resident.tile([P, RUN, D], F32, name="out_chunk%d" % c)
-            for j in range(RUN):
-                nc.vector.tensor_tensor(
-                    out=out_chunk[:, j, :], in0=x_chunks[c][:, j, :], in1=bias_psum[:], op=ADD
+        def flip_class():
+            cls_flipped = psum_flip.tile([P, 2, P], F32, tag="flipped")
+            transpose_words(nc, cls_flipped, cls_ctx[:], ident[:])
+            cls_grouped = const.tile([P, P, PACK], BF16, align_bytes=64)
+            nc.scalar.copy(
+                out=cls_grouped[:].bitcast(F32), in_=cls_flipped[:].rearrange("q u n -> q n u")
+            )
+            nc.vector.quantize_mx(
+                out=cls_codes[:].bitcast(FP8X4),
+                scales=cls_scales[:],
+                in_=cls_grouped[:].rearrange("q n v -> q (n v)"),
+            )
+
+        def multiply_class():
+            cls_prod = psum_prod.tile([P, D_TILES, P], F32, tag="prod")
+            for m in range(D_TILES):
+                multiply_by_w(cls_prod[:, m, :], m, cls_codes[:], cls_scales[:])
+            cls_sum = const.tile([P, D_TILES, SAMPLES], F32)
+            nc.vector.tensor_reduce(
+                out=cls_sum[:],
+                in_=cls_prod[:].rearrange("i m (b t) -> i m b t", t=FRAMES),
+                axis=mybir.AxisListType.X,
+                op=ADD,
+            )
+            for m in range(D_TILES):
+                nc.scalar.activation(
+                    out=cls_mean[:, m, 0:SAMPLES],
+                    in_=cls_sum[:, m, :],
+                    func=IDENTITY,
+                    bias=bias_col[:, m : m + 1],
+                    scale=1.0 / FRAMES,
                 )
 
+        def finish_class():
+            cls_back = psum_back.tile([P, D], F32, tag="back")
+            for m in range(D_TILES):
+                nc.tensor.transpose(cls_back[:, m * P : (m + 1) * P], cls_mean[:, m, :], ident[:])
+            cls_out = const.tile([SAMPLES, D], F32)
+            nc.vector.tensor_tensor(
+                out=cls_out[:], in0=cls_back[0:SAMPLES, :], in1=cls_x[:], op=ADD
+            )
+            nc.sync.dma_start(out=out[:, 0, :], in_=cls_out[:])
+
+        quantised = {}
+        biased = {}
+
+        def flip(c):
             grouped = work.tile(
                 [P, RUN * SAMPLES, CHUNK_PATCHES, FRAME_GROUPS, PACK], BF16, align_bytes=64
             )
@@ -156,24 +180,46 @@ def tile_timesformerlayer_pc_t_kernel(tc, ctx_s, x_res, s_out_w, s_out_b, out):
             for pair in range(CHUNK_PATCHES // 2):
                 flipped = psum_flip.tile([P, 2, 2, P], F32, tag="flipped")
                 for i in range(2):
-                    a = 2 * pair + i
-                    transpose_words(nc, flipped[:, i], ctx_chunks[c][:, a, :], by_row[:])
+                    transpose_words(nc, flipped[:, i], ctx_chunks[c][:, 2 * pair + i, :], by_row[:])
+                for i in range(2):
                     nc.scalar.copy(
-                        out=grouped_words[:, :, a, :, :],
-                        in_=flipped[:, i].rearrange("q u (m h) -> q m h u", h=FRAME_GROUPS),
+                        out=grouped_words[:, :, 2 * pair + i, :, :],
+                        in_=flipped[:, i].rearrange("q u (r h) -> q r h u", h=FRAME_GROUPS),
                     )
-            codes = work.tile([P, RUN * P], U32, align_bytes=64)
-            scales = work.tile([P, RUN * P], U8, align_bytes=64)
+            codes = work.tile([P, CHUNK_TOKENS], U32, align_bytes=64)
+            scales = work.tile([P, CHUNK_TOKENS], U8, align_bytes=64)
             nc.vector.quantize_mx(
                 out=codes[:].bitcast(FP8X4),
                 scales=scales[:],
-                in_=grouped[:].rearrange("q m a h v -> q (m a h v)"),
+                in_=grouped[:].rearrange("q r a h v -> q (r a h v)"),
             )
+            quantised[c] = (codes, scales)
+
+        def multiply(c):
+            codes, scales = quantised[c]
+            with_bias = work.tile([P, D_TILES, CHUNK_TOKENS], F32)
+            for m in range(D_TILES):
+                prod = psum_prod.tile([P, CHUNK_TOKENS], F32, tag="prod")
+                multiply_by_w(prod[:], m, codes[:], scales[:])
+                nc.scalar.activation(
+                    out=with_bias[:, m, :],
+                    in_=prod[:],
+                    func=IDENTITY,
+                    bias=bias_col[:, m : m + 1],
+                    scale=1.0,
+                )
+            biased[c] = with_bias
+
+        def finish(c):
+            out_chunk = resident.tile([P, RUN, D], F32, name="out_chunk%d" % c)
             for j in range(RUN):
-                tokens = slice(j * P, (j + 1) * P)
-                prod = product(codes[:, tokens], scales[:, tokens])
+                back = psum_back.tile([P, D], F32, tag="back")
+                for m in range(D_TILES):
+                    nc.tensor.transpose(
+                        back[:, m * P : (m + 1) * P], biased[c][:, m, j * P : (j + 1) * P], ident[:]
+                    )
                 nc.vector.tensor_tensor(
-                    out=out_chunk[:, j, :], in0=prod[:], in1=out_chunk[:, j, :], op=ADD
+                    out=out_chunk[:, j, :], in0=back[:], in1=x_chunks[c][:, j, :], op=ADD
                 )
             first_row = 1 + c * CHUNK_ROWS
             nc.sync.dma_start(
@@ -182,3 +228,17 @@ def tile_timesformerlayer_pc_t_kernel(tc, ctx_s, x_res, s_out_w, s_out_b, out):
                 ),
                 in_=out_chunk[:].rearrange("p j d -> p (j d)"),
             )
+
+        flip_class()
+        flip(0)
+        multiply_class()
+        flip(1)
+        multiply(0)
+        finish_class()
+        for c in range(2, CHUNKS):
+            flip(c)
+            multiply(c - 1)
+            finish(c - 2)
+        multiply(CHUNKS - 1)
+        finish(CHUNKS - 2)
+        finish(CHUNKS - 1)

@@ -19,12 +19,18 @@ PATCHES = 36
 D = 512
 D_TILES = D // P
 
-RUN = 4
-CHUNK_ROWS = (P // SAMPLES) * RUN
-CHUNK_PATCHES = CHUNK_ROWS // FRAMES
-CHUNK_TOKENS = RUN * P
+CHUNK_PATCHES = 4
 CHUNKS = PATCHES // CHUNK_PATCHES
-FRAME_GROUPS = FRAMES // RUN
+GROUP_TILES = 4
+GROUP_TOKENS = GROUP_TILES * P
+
+MAIN_RUN = 2
+MAIN_ROWS = P * MAIN_RUN
+MAIN_CHUNKS = MAIN_ROWS // FRAMES // CHUNK_PATCHES
+GROUP_SAMPLES = GROUP_TILES // MAIN_RUN
+MAIN_GROUPS = SAMPLES // GROUP_SAMPLES
+TAIL_RUN = 4
+TAIL = MAIN_GROUPS
 
 FLOPS = 2 * SAMPLES * FRAMES * (1 + PATCHES) * D * D
 
@@ -35,16 +41,32 @@ def transpose_words(nc, flipped, rows, permutation):
         nc.tensor.transpose(flipped[:, u, :], words[:, u * P : (u + 1) * P], permutation)
 
 
+def rows_in_hbm(tensor, g):
+    if g == TAIL:
+        return tensor[:, 1 + MAIN_ROWS :, :].rearrange("b (x j) d -> b x (j d)", j=TAIL_RUN)
+    samples = tensor[g * GROUP_SAMPLES : (g + 1) * GROUP_SAMPLES, 1 : 1 + MAIN_ROWS, :]
+    return samples.rearrange("s (p j) d -> p s (j d)", j=MAIN_RUN)
+
+
+def rows_in_sbuf(tiles, g):
+    if g == TAIL:
+        return tiles[:].rearrange("p j d -> p (j d)")
+    return tiles[:].rearrange("p (s j) d -> p s (j d)", j=MAIN_RUN)
+
+
 def tile_timesformerlayer_pc_t_kernel(tc, ctx_s, x_res, s_out_w, s_out_b, out):
     nc = tc.nc
     with ExitStack() as scope:
         const = scope.enter_context(tc.tile_pool(name="const", bufs=1))
         resident = scope.enter_context(tc.tile_pool(name="resident", bufs=1))
         work = scope.enter_context(tc.tile_pool(name="work", bufs=3))
+        stores = scope.enter_context(tc.tile_pool(name="stores", bufs=4))
         psum_flip = scope.enter_context(tc.psum_pool(name="psum_flip", bufs=2))
         psum_prod = scope.enter_context(tc.psum_pool(name="psum_prod", bufs=3))
         psum_back = scope.enter_context(tc.psum_pool(name="psum_back", bufs=3))
         scope.enter_context(tc.manual_schedule())
+
+        group_order = [TAIL] + list(range(MAIN_GROUPS))
 
         bias_rows = const.tile([P, P], BF16)
         nc.vector.memset(bias_rows[:], 0.0)
@@ -60,39 +82,31 @@ def tile_timesformerlayer_pc_t_kernel(tc, ctx_s, x_res, s_out_w, s_out_b, out):
         nc.sync.dma_start(out=cls_ctx[:], in_=ctx_s[:, 0, :])
         cls_x = resident.tile([SAMPLES, D], BF16)
         nc.sync.dma_start(out=cls_x[:], in_=x_res[:, 0, :])
-        ctx_chunks = []
-        x_chunks = []
-
-        def load_x(c):
-            x_chunk = resident.tile([P, RUN, D], BF16, name="x_chunk%d" % c)
-            first_row = 1 + c * CHUNK_ROWS
-            nc.sync.dma_start(
-                out=x_chunk[:].rearrange("p j d -> p (j d)"),
-                in_=x_res[:, first_row : first_row + CHUNK_ROWS, :].rearrange(
-                    "b (x j) d -> b x (j d)", j=RUN
-                ),
-            )
-            x_chunks.append(x_chunk)
-
-        for c in range(CHUNKS):
+        ctx_chunks = {}
+        for c in group_order:
             ctx_chunk = resident.tile([P, CHUNK_PATCHES, D], BF16, name="ctx_chunk%d" % c)
-            first_patch = 1 + c * CHUNK_PATCHES
-            nc.sync.dma_start(
-                out=ctx_chunk[:], in_=ctx_s[:, first_patch : first_patch + CHUNK_PATCHES, :]
-            )
-            ctx_chunks.append(ctx_chunk)
-            if c >= 1:
-                load_x(c - 1)
-        load_x(CHUNKS - 1)
+            first = 1 + c * CHUNK_PATCHES
+            nc.sync.dma_start(out=ctx_chunk[:], in_=ctx_s[:, first : first + CHUNK_PATCHES, :])
+            ctx_chunks[c] = ctx_chunk
+        x_groups = {}
+        for g in group_order:
+            x_group = resident.tile([P, GROUP_TILES, D], BF16, name="x_group%d" % g)
+            nc.sync.dma_start(out=rows_in_sbuf(x_group, g), in_=rows_in_hbm(x_res, g))
+            x_groups[g] = x_group
 
         ident = const.tile([P, P], F32)
         make_identity(nc, ident[:])
         ident_bf16 = const.tile([P, P], BF16)
         nc.vector.tensor_copy(out=ident_bf16[:], in_=ident[:])
-        by_row = const.tile([P, P], F32)
+        main_order = const.tile([P, P], F32)
         nc.vector.tensor_copy(
-            out=by_row[:].rearrange("n (j g) -> n j g", j=RUN),
-            in_=ident[:].rearrange("n (g j) -> n j g", j=RUN),
+            out=main_order[:].rearrange("n (b j h) -> n b j h", j=MAIN_RUN, h=FRAMES // MAIN_RUN),
+            in_=ident[:].rearrange("n (b h j) -> n b j h", j=MAIN_RUN, h=FRAMES // MAIN_RUN),
+        )
+        tail_order = const.tile([P, P], F32)
+        nc.vector.tensor_copy(
+            out=tail_order[:].rearrange("n (j g) -> n j g", j=TAIL_RUN),
+            in_=ident[:].rearrange("n (g j) -> n j g", j=TAIL_RUN),
         )
         bias_flipped = psum_back.tile([P, P], BF16, tag="back")
         nc.tensor.transpose(bias_flipped[:], bias_rows[:], ident_bf16[:])
@@ -169,37 +183,53 @@ def tile_timesformerlayer_pc_t_kernel(tc, ctx_s, x_res, s_out_w, s_out_b, out):
             )
             nc.sync.dma_start(out=out[:, 0, :], in_=cls_out[:])
 
+        main_tokens = resident.tile([P, SAMPLES * MAIN_RUN, P, PACK], BF16, align_bytes=64)
+        main_words = main_tokens[:].bitcast(F32)
+        tail_tokens = resident.tile(
+            [P, TAIL_RUN * SAMPLES, CHUNK_PATCHES, FRAMES // TAIL_RUN, PACK], BF16, align_bytes=64
+        )
+        tail_words = tail_tokens[:].bitcast(F32)
+
+        def flip(c):
+            for half in range(2):
+                flipped = psum_flip.tile([P, 2, 2, P], F32, tag="flipped")
+                for i in range(2):
+                    a = 2 * half + i
+                    order = tail_order if c == TAIL else main_order
+                    transpose_words(nc, flipped[:, i], ctx_chunks[c][:, a, :], order[:])
+                for i in range(2):
+                    a = 2 * half + i
+                    if c == TAIL:
+                        sorted_tokens = flipped[:, i].rearrange("q u (r h) -> q r h u", h=2)
+                        place = tail_words[:, :, a, :, :]
+                    else:
+                        sorted_tokens = flipped[:, i].rearrange("q u (r h) -> q r h u", h=4)
+                        first = 4 * (c * CHUNK_PATCHES + a)
+                        place = main_words[:, :, first : first + 4, :]
+                    if half == 0:
+                        nc.scalar.copy(out=place, in_=sorted_tokens)
+                    else:
+                        nc.vector.tensor_copy(out=place, in_=sorted_tokens)
+
         quantised = {}
         biased = {}
 
-        def flip(c):
-            grouped = work.tile(
-                [P, RUN * SAMPLES, CHUNK_PATCHES, FRAME_GROUPS, PACK], BF16, align_bytes=64
-            )
-            grouped_words = grouped[:].bitcast(F32)
-            for pair in range(CHUNK_PATCHES // 2):
-                flipped = psum_flip.tile([P, 2, 2, P], F32, tag="flipped")
-                for i in range(2):
-                    transpose_words(nc, flipped[:, i], ctx_chunks[c][:, 2 * pair + i, :], by_row[:])
-                for i in range(2):
-                    nc.scalar.copy(
-                        out=grouped_words[:, :, 2 * pair + i, :, :],
-                        in_=flipped[:, i].rearrange("q u (r h) -> q r h u", h=FRAME_GROUPS),
-                    )
-            codes = work.tile([P, CHUNK_TOKENS], U32, align_bytes=64)
-            scales = work.tile([P, CHUNK_TOKENS], U8, align_bytes=64)
-            nc.vector.quantize_mx(
-                out=codes[:].bitcast(FP8X4),
-                scales=scales[:],
-                in_=grouped[:].rearrange("q r a h v -> q (r a h v)"),
-            )
-            quantised[c] = (codes, scales)
+        def quantise(g):
+            if g == TAIL:
+                tokens = tail_tokens[:].rearrange("q r a h v -> q (r a h v)")
+            else:
+                tiles = main_tokens[:, g * GROUP_TILES : (g + 1) * GROUP_TILES, :, :]
+                tokens = tiles.rearrange("q r p v -> q (r p v)")
+            codes = work.tile([P, GROUP_TOKENS], U32, align_bytes=64)
+            scales = work.tile([P, GROUP_TOKENS], U8, align_bytes=64)
+            nc.vector.quantize_mx(out=codes[:].bitcast(FP8X4), scales=scales[:], in_=tokens)
+            quantised[g] = (codes, scales)
 
-        def multiply(c):
-            codes, scales = quantised[c]
-            with_bias = work.tile([P, D_TILES, CHUNK_TOKENS], F32)
+        def multiply(g):
+            codes, scales = quantised[g]
+            with_bias = work.tile([P, D_TILES, GROUP_TOKENS], F32)
             for m in range(D_TILES):
-                prod = psum_prod.tile([P, CHUNK_TOKENS], F32, tag="prod")
+                prod = psum_prod.tile([P, GROUP_TOKENS], F32, tag="prod")
                 multiply_by_w(prod[:], m, codes[:], scales[:])
                 nc.scalar.activation(
                     out=with_bias[:, m, :],
@@ -208,37 +238,36 @@ def tile_timesformerlayer_pc_t_kernel(tc, ctx_s, x_res, s_out_w, s_out_b, out):
                     bias=bias_col[:, m : m + 1],
                     scale=1.0,
                 )
-            biased[c] = with_bias
+            biased[g] = with_bias
 
-        def finish(c):
-            out_chunk = resident.tile([P, RUN, D], F32, name="out_chunk%d" % c)
-            for j in range(RUN):
+        def finish(g):
+            out_group = stores.tile([P, GROUP_TILES, D], F32)
+            for i in range(GROUP_TILES):
                 back = psum_back.tile([P, D], F32, tag="back")
                 for m in range(D_TILES):
                     nc.tensor.transpose(
-                        back[:, m * P : (m + 1) * P], biased[c][:, m, j * P : (j + 1) * P], ident[:]
+                        back[:, m * P : (m + 1) * P], biased[g][:, m, i * P : (i + 1) * P], ident[:]
                     )
                 nc.vector.tensor_tensor(
-                    out=out_chunk[:, j, :], in0=back[:], in1=x_chunks[c][:, j, :], op=ADD
+                    out=out_group[:, i, :], in0=back[:], in1=x_groups[g][:, i, :], op=ADD
                 )
-            first_row = 1 + c * CHUNK_ROWS
-            nc.sync.dma_start(
-                out=out[:, first_row : first_row + CHUNK_ROWS, :].rearrange(
-                    "b (x j) d -> b x (j d)", j=RUN
-                ),
-                in_=out_chunk[:].rearrange("p j d -> p (j d)"),
-            )
+            nc.sync.dma_start(out=rows_in_hbm(out, g), in_=rows_in_sbuf(out_group, g))
 
         flip_class()
+        flip(TAIL)
+        quantise(TAIL)
         flip(0)
         multiply_class()
         flip(1)
-        multiply(0)
+        multiply(TAIL)
+        flip(2)
         finish_class()
-        for c in range(2, CHUNKS):
+        for c in range(3, MAIN_CHUNKS):
             flip(c)
-            multiply(c - 1)
-            finish(c - 2)
-        multiply(CHUNKS - 1)
-        finish(CHUNKS - 2)
-        finish(CHUNKS - 1)
+        quantise(group_order[1])
+        for k in range(1, len(group_order)):
+            if k + 1 < len(group_order):
+                quantise(group_order[k + 1])
+            multiply(group_order[k])
+            finish(group_order[k - 1])
+        finish(group_order[len(group_order) - 1])

@@ -213,6 +213,7 @@ def tile_timesformerlayer_pc_t_kernel(tc, ctx_s, x_res, s_out_w, s_out_b, out):
 
         quantised = {}
         biased = {}
+        finished = {}
 
         def quantise(g):
             if g == TAIL:
@@ -224,34 +225,33 @@ def tile_timesformerlayer_pc_t_kernel(tc, ctx_s, x_res, s_out_w, s_out_b, out):
             scales = work.tile([P, GROUP_TOKENS], U8, align_bytes=64)
             nc.vector.quantize_mx(out=codes[:].bitcast(FP8X4), scales=scales[:], in_=tokens)
             quantised[g] = (codes, scales)
+            biased[g] = work.tile([P, D_TILES, GROUP_TOKENS], F32, name="with_bias")
+            finished[g] = stores.tile([P, GROUP_TILES, D], F32, name="out_group")
 
-        def multiply(g):
+        def multiply(g, m):
             codes, scales = quantised[g]
-            with_bias = work.tile([P, D_TILES, GROUP_TOKENS], F32)
-            for m in range(D_TILES):
-                prod = psum_prod.tile([P, GROUP_TOKENS], F32, tag="prod")
-                multiply_by_w(prod[:], m, codes[:], scales[:])
-                nc.scalar.activation(
-                    out=with_bias[:, m, :],
-                    in_=prod[:],
-                    func=IDENTITY,
-                    bias=bias_col[:, m : m + 1],
-                    scale=1.0,
-                )
-            biased[g] = with_bias
+            prod = psum_prod.tile([P, GROUP_TOKENS], F32, tag="prod")
+            multiply_by_w(prod[:], m, codes[:], scales[:])
+            nc.scalar.activation(
+                out=biased[g][:, m, :],
+                in_=prod[:],
+                func=IDENTITY,
+                bias=bias_col[:, m : m + 1],
+                scale=1.0,
+            )
 
-        def finish(g):
-            out_group = stores.tile([P, GROUP_TILES, D], F32)
-            for i in range(GROUP_TILES):
-                back = psum_back.tile([P, D], F32, tag="back")
-                for m in range(D_TILES):
-                    nc.tensor.transpose(
-                        back[:, m * P : (m + 1) * P], biased[g][:, m, i * P : (i + 1) * P], ident[:]
-                    )
-                nc.vector.tensor_tensor(
-                    out=out_group[:, i, :], in0=back[:], in1=x_groups[g][:, i, :], op=ADD
+        def finish(g, i):
+            back = psum_back.tile([P, D], F32, tag="back")
+            for m in range(D_TILES):
+                nc.tensor.transpose(
+                    back[:, m * P : (m + 1) * P], biased[g][:, m, i * P : (i + 1) * P], ident[:]
                 )
-            nc.sync.dma_start(out=rows_in_hbm(out, g), in_=rows_in_sbuf(out_group, g))
+            nc.vector.tensor_tensor(
+                out=finished[g][:, i, :], in0=back[:], in1=x_groups[g][:, i, :], op=ADD
+            )
+
+        def store(g):
+            nc.sync.dma_start(out=rows_in_hbm(out, g), in_=rows_in_sbuf(finished[g], g))
 
         flip_class()
         flip(TAIL)
@@ -259,7 +259,8 @@ def tile_timesformerlayer_pc_t_kernel(tc, ctx_s, x_res, s_out_w, s_out_b, out):
         flip(0)
         multiply_class()
         flip(1)
-        multiply(TAIL)
+        for m in range(D_TILES):
+            multiply(TAIL, m)
         flip(2)
         finish_class()
         for c in range(3, MAIN_CHUNKS):
@@ -268,6 +269,11 @@ def tile_timesformerlayer_pc_t_kernel(tc, ctx_s, x_res, s_out_w, s_out_b, out):
         for k in range(1, len(group_order)):
             if k + 1 < len(group_order):
                 quantise(group_order[k + 1])
-            multiply(group_order[k])
-            finish(group_order[k - 1])
-        finish(group_order[len(group_order) - 1])
+            for i in range(GROUP_TILES):
+                multiply(group_order[k], i)
+                finish(group_order[k - 1], i)
+            store(group_order[k - 1])
+        last = group_order[len(group_order) - 1]
+        for i in range(GROUP_TILES):
+            finish(last, i)
+        store(last)

@@ -9,7 +9,6 @@ U32 = mybir.dt.uint32
 U8 = mybir.dt.uint8
 FP8X4 = mybir.dt.float8_e4m3fn_x4
 ADD = mybir.AluOpType.add
-IDENTITY = mybir.ActivationFunctionType.Identity
 
 P = 128
 PACK = 4
@@ -17,20 +16,14 @@ SAMPLES = 16
 FRAMES = 8
 PATCHES = 36
 D = 512
-D_TILES = D // P
 
-CHUNK_PATCHES = 4
+RUN = 4
+CHUNK_ROWS = (P // SAMPLES) * RUN
+CHUNK_PATCHES = CHUNK_ROWS // FRAMES
 CHUNKS = PATCHES // CHUNK_PATCHES
-GROUP_TILES = 4
-GROUP_TOKENS = GROUP_TILES * P
+FRAME_GROUPS = FRAMES // RUN
 
-MAIN_RUN = 2
-MAIN_ROWS = P * MAIN_RUN
-MAIN_CHUNKS = MAIN_ROWS // FRAMES // CHUNK_PATCHES
-GROUP_SAMPLES = GROUP_TILES // MAIN_RUN
-MAIN_GROUPS = SAMPLES // GROUP_SAMPLES
-TAIL_RUN = 4
-TAIL = MAIN_GROUPS
+GPSIMD_TILES = 3
 
 FLOPS = 2 * SAMPLES * FRAMES * (1 + PATCHES) * D * D
 
@@ -41,38 +34,17 @@ def transpose_words(nc, flipped, rows, permutation):
         nc.tensor.transpose(flipped[:, u, :], words[:, u * P : (u + 1) * P], permutation)
 
 
-def rows_in_hbm(tensor, g):
-    if g == TAIL:
-        return tensor[:, 1 + MAIN_ROWS :, :].rearrange("b (x j) d -> b x (j d)", j=TAIL_RUN)
-    samples = tensor[g * GROUP_SAMPLES : (g + 1) * GROUP_SAMPLES, 1 : 1 + MAIN_ROWS, :]
-    return samples.rearrange("s (p j) d -> p s (j d)", j=MAIN_RUN)
-
-
-def rows_in_sbuf(tiles, g):
-    if g == TAIL:
-        return tiles[:].rearrange("p j d -> p (j d)")
-    return tiles[:].rearrange("p (s j) d -> p s (j d)", j=MAIN_RUN)
-
-
 def tile_timesformerlayer_pc_t_kernel(tc, ctx_s, x_res, s_out_w, s_out_b, out):
     nc = tc.nc
-    with ExitStack() as scope:
-        const = scope.enter_context(tc.tile_pool(name="const", bufs=1))
-        resident = scope.enter_context(tc.tile_pool(name="resident", bufs=1))
-        work = scope.enter_context(tc.tile_pool(name="work", bufs=3))
-        stores = scope.enter_context(tc.tile_pool(name="stores", bufs=4))
-        psum_flip = scope.enter_context(tc.psum_pool(name="psum_flip", bufs=2))
-        psum_prod = scope.enter_context(tc.psum_pool(name="psum_prod", bufs=3))
-        psum_back = scope.enter_context(tc.psum_pool(name="psum_back", bufs=3))
-        scope.enter_context(tc.manual_schedule())
+    with ExitStack() as pools:
+        const = pools.enter_context(tc.tile_pool(name="const", bufs=1))
+        resident = pools.enter_context(tc.tile_pool(name="resident", bufs=1))
+        work = pools.enter_context(tc.tile_pool(name="work", bufs=3))
+        sums = pools.enter_context(tc.tile_pool(name="sums", bufs=4))
+        psum_bias = pools.enter_context(tc.psum_pool(name="psum_bias", bufs=1))
+        psum_flip = pools.enter_context(tc.psum_pool(name="psum_flip", bufs=3))
+        psum_prod = pools.enter_context(tc.psum_pool(name="psum_prod", bufs=4))
 
-        group_order = [TAIL] + list(range(MAIN_GROUPS))
-
-        bias_rows = const.tile([P, P], BF16)
-        nc.vector.memset(bias_rows[:], 0.0)
-        nc.sync.dma_start(
-            out=bias_rows[0:D_TILES, :], in_=s_out_b.rearrange("(m d) -> m d", m=D_TILES)
-        )
         w_rows = const.tile([P, PACK, D], BF16)
         nc.sync.dma_start(
             out=w_rows[:].rearrange("q (u e) c -> q u (e c)", u=2),
@@ -80,38 +52,54 @@ def tile_timesformerlayer_pc_t_kernel(tc, ctx_s, x_res, s_out_w, s_out_b, out):
         )
         cls_ctx = resident.tile([P, D], BF16)
         nc.sync.dma_start(out=cls_ctx[:], in_=ctx_s[:, 0, :])
+        bias_row = const.tile([P, D], BF16)
+        nc.vector.memset(bias_row[:], 0.0)
+        nc.sync.dma_start(out=bias_row[0:1, :], in_=s_out_b.rearrange("(o d) -> o d", o=1))
         cls_x = resident.tile([SAMPLES, D], BF16)
         nc.sync.dma_start(out=cls_x[:], in_=x_res[:, 0, :])
-        ctx_chunks = {}
-        for c in group_order:
+        ctx_chunks = []
+        x_chunks = []
+        for c in range(CHUNKS):
             ctx_chunk = resident.tile([P, CHUNK_PATCHES, D], BF16, name="ctx_chunk%d" % c)
-            first = 1 + c * CHUNK_PATCHES
-            nc.sync.dma_start(out=ctx_chunk[:], in_=ctx_s[:, first : first + CHUNK_PATCHES, :])
-            ctx_chunks[c] = ctx_chunk
-        x_groups = {}
-        for g in group_order:
-            x_group = resident.tile([P, GROUP_TILES, D], BF16, name="x_group%d" % g)
-            nc.sync.dma_start(out=rows_in_sbuf(x_group, g), in_=rows_in_hbm(x_res, g))
-            x_groups[g] = x_group
+            first_patch = 1 + c * CHUNK_PATCHES
+            nc.sync.dma_start(
+                out=ctx_chunk[:], in_=ctx_s[:, first_patch : first_patch + CHUNK_PATCHES, :]
+            )
+            ctx_chunks.append(ctx_chunk)
+            x_chunk = resident.tile([P, RUN, D], BF16, name="x_chunk%d" % c)
+            first_row = 1 + c * CHUNK_ROWS
+            nc.sync.dma_start(
+                out=x_chunk[:].rearrange("p j d -> p (j d)"),
+                in_=x_res[:, first_row : first_row + CHUNK_ROWS, :].rearrange(
+                    "b (x j) d -> b x (j d)", j=RUN
+                ),
+            )
+            x_chunks.append(x_chunk)
 
         ident = const.tile([P, P], F32)
         make_identity(nc, ident[:])
-        ident_bf16 = const.tile([P, P], BF16)
-        nc.vector.tensor_copy(out=ident_bf16[:], in_=ident[:])
-        main_order = const.tile([P, P], F32)
+        by_row = const.tile([P, P], F32)
         nc.vector.tensor_copy(
-            out=main_order[:].rearrange("n (b j h) -> n b j h", j=MAIN_RUN, h=FRAMES // MAIN_RUN),
-            in_=ident[:].rearrange("n (b h j) -> n b j h", j=MAIN_RUN, h=FRAMES // MAIN_RUN),
+            out=by_row[:].rearrange("n (j g) -> n j g", j=RUN),
+            in_=ident[:].rearrange("n (g j) -> n j g", j=RUN),
         )
-        tail_order = const.tile([P, P], F32)
-        nc.vector.tensor_copy(
-            out=tail_order[:].rearrange("n (j g) -> n j g", j=TAIL_RUN),
-            in_=ident[:].rearrange("n (g j) -> n j g", j=TAIL_RUN),
+        frame_mean = const.tile([P, P], F32)
+        nc.vector.memset(frame_mean[:], 0.0)
+        nc.vector.tensor_reduce(
+            out=frame_mean[:, 0:SAMPLES],
+            in_=ident[:].rearrange("n (b t) -> n b t", t=FRAMES),
+            axis=mybir.AxisListType.X,
+            op=ADD,
         )
-        bias_flipped = psum_back.tile([P, P], BF16, tag="back")
-        nc.tensor.transpose(bias_flipped[:], bias_rows[:], ident_bf16[:])
-        bias_col = const.tile([P, D_TILES], F32)
-        nc.scalar.copy(out=bias_col[:], in_=bias_flipped[:, 0:D_TILES])
+        nc.vector.tensor_scalar_mul(
+            out=frame_mean[:, 0:SAMPLES], in0=frame_mean[:, 0:SAMPLES], scalar1=1.0 / FRAMES
+        )
+        ones = const.tile([P, P], BF16)
+        nc.vector.memset(ones[:], 1.0)
+        bias_psum = psum_bias.tile([P, D], F32)
+        nc.tensor.matmul(out=bias_psum[:], lhsT=ones[:], rhs=bias_row[:], start=True, stop=True)
+        bias_sbuf = const.tile([P, D], F32)
+        nc.scalar.copy(out=bias_sbuf[:], in_=bias_psum[:])
 
         w_grouped = const.tile([P, D, PACK], BF16, align_bytes=64)
         nc.vector.tensor_copy(out=w_grouped[:], in_=w_rows[:].rearrange("q v c -> q c v"))
@@ -123,157 +111,86 @@ def tile_timesformerlayer_pc_t_kernel(tc, ctx_s, x_res, s_out_w, s_out_b, out):
             in_=w_grouped[:].rearrange("q c v -> q (c v)"),
         )
 
-        def multiply_by_w(prod, m, codes, scales):
-            columns = slice(m * P, (m + 1) * P)
+        def product(codes, scales):
+            prod = psum_prod.tile([P, D], F32, tag="prod")
             nc.tensor.matmul_mx(
-                out=prod,
-                lhsT=w_codes[:, columns].bitcast(FP8X4),
-                lhsT_scale=w_scales[:, columns],
-                rhs=codes.bitcast(FP8X4),
-                rhs_scale=scales,
+                out=prod[:],
+                lhsT=codes.bitcast(FP8X4),
+                lhsT_scale=scales,
+                rhs=w_codes[:].bitcast(FP8X4),
+                rhs_scale=w_scales[:],
                 start=True,
                 stop=True,
             )
+            return prod
 
+        cls_flipped = psum_flip.tile([P, 2, P], F32, tag="flipped")
+        transpose_words(nc, cls_flipped, cls_ctx[:], ident[:])
+        cls_grouped = const.tile([P, P, PACK], BF16, align_bytes=64)
+        nc.scalar.copy(
+            out=cls_grouped[:].bitcast(F32), in_=cls_flipped[:].rearrange("q u n -> q n u")
+        )
         cls_codes = const.tile([P, P], U32, align_bytes=64)
         cls_scales = const.tile([P, P], U8, align_bytes=64)
-        cls_mean = const.tile([P, D_TILES, P], F32)
-        nc.vector.memset(cls_mean[:], 0.0)
+        nc.vector.quantize_mx(
+            out=cls_codes[:].bitcast(FP8X4),
+            scales=cls_scales[:],
+            in_=cls_grouped[:].rearrange("q n v -> q (n v)"),
+        )
+        cls_prod = product(cls_codes[:], cls_scales[:])
+        cls_res = const.tile([P, D], F32)
+        nc.scalar.copy(out=cls_res[:], in_=cls_prod[:])
+        cls_mean = psum_prod.tile([P, D], F32, tag="prod")
+        nc.tensor.matmul(out=cls_mean[:], lhsT=frame_mean[:], rhs=cls_res[:], start=True, stop=True)
+        cls_out = const.tile([SAMPLES, D], F32)
+        nc.vector.tensor_tensor(out=cls_out[:], in0=cls_x[:], in1=bias_psum[0:SAMPLES, :], op=ADD)
+        nc.vector.tensor_tensor(out=cls_out[:], in0=cls_mean[0:SAMPLES, :], in1=cls_out[:], op=ADD)
+        nc.sync.dma_start(out=out[:, 0, :], in_=cls_out[:])
 
-        def flip_class():
-            cls_flipped = psum_flip.tile([P, 2, P], F32, tag="flipped")
-            transpose_words(nc, cls_flipped, cls_ctx[:], ident[:])
-            cls_grouped = const.tile([P, P, PACK], BF16, align_bytes=64)
-            nc.scalar.copy(
-                out=cls_grouped[:].bitcast(F32), in_=cls_flipped[:].rearrange("q u n -> q n u")
-            )
-            nc.vector.quantize_mx(
-                out=cls_codes[:].bitcast(FP8X4),
-                scales=cls_scales[:],
-                in_=cls_grouped[:].rearrange("q n v -> q (n v)"),
-            )
-
-        def multiply_class():
-            cls_prod = psum_prod.tile([P, D_TILES, P], F32, tag="prod")
-            for m in range(D_TILES):
-                multiply_by_w(cls_prod[:, m, :], m, cls_codes[:], cls_scales[:])
-            cls_sum = const.tile([P, D_TILES, SAMPLES], F32)
-            nc.vector.tensor_reduce(
-                out=cls_sum[:],
-                in_=cls_prod[:].rearrange("i m (b t) -> i m b t", t=FRAMES),
-                axis=mybir.AxisListType.X,
+        for c in range(CHUNKS):
+            x_biased = sums.tile([P, RUN, D], F32)
+            nc.gpsimd.tensor_tensor(
+                out=x_biased[:, 0:GPSIMD_TILES, :],
+                in0=x_chunks[c][:, 0:GPSIMD_TILES, :],
+                in1=bias_sbuf[:].unsqueeze(1).to_broadcast([P, GPSIMD_TILES, D]),
                 op=ADD,
             )
-            for m in range(D_TILES):
-                nc.scalar.activation(
-                    out=cls_mean[:, m, 0:SAMPLES],
-                    in_=cls_sum[:, m, :],
-                    func=IDENTITY,
-                    bias=bias_col[:, m : m + 1],
-                    scale=1.0 / FRAMES,
+            for j in range(GPSIMD_TILES, RUN):
+                nc.vector.tensor_tensor(
+                    out=x_biased[:, j, :], in0=x_chunks[c][:, j, :], in1=bias_psum[:], op=ADD
                 )
 
-        def finish_class():
-            cls_back = psum_back.tile([P, D], F32, tag="back")
-            for m in range(D_TILES):
-                nc.tensor.transpose(cls_back[:, m * P : (m + 1) * P], cls_mean[:, m, :], ident[:])
-            cls_out = const.tile([SAMPLES, D], F32)
-            nc.vector.tensor_tensor(
-                out=cls_out[:], in0=cls_back[0:SAMPLES, :], in1=cls_x[:], op=ADD
+            grouped = work.tile(
+                [P, RUN * SAMPLES, CHUNK_PATCHES, FRAME_GROUPS, PACK], BF16, align_bytes=64
             )
-            nc.sync.dma_start(out=out[:, 0, :], in_=cls_out[:])
-
-        main_tokens = resident.tile([P, SAMPLES * MAIN_RUN, P, PACK], BF16, align_bytes=64)
-        main_words = main_tokens[:].bitcast(F32)
-        tail_tokens = resident.tile(
-            [P, TAIL_RUN * SAMPLES, CHUNK_PATCHES, FRAMES // TAIL_RUN, PACK], BF16, align_bytes=64
-        )
-        tail_words = tail_tokens[:].bitcast(F32)
-
-        def flip(c):
-            for half in range(2):
+            grouped_words = grouped[:].bitcast(F32)
+            for pair in range(CHUNK_PATCHES // 2):
                 flipped = psum_flip.tile([P, 2, 2, P], F32, tag="flipped")
                 for i in range(2):
-                    a = 2 * half + i
-                    order = tail_order if c == TAIL else main_order
-                    transpose_words(nc, flipped[:, i], ctx_chunks[c][:, a, :], order[:])
-                for i in range(2):
-                    a = 2 * half + i
-                    if c == TAIL:
-                        sorted_tokens = flipped[:, i].rearrange("q u (r h) -> q r h u", h=2)
-                        place = tail_words[:, :, a, :, :]
-                    else:
-                        sorted_tokens = flipped[:, i].rearrange("q u (r h) -> q r h u", h=4)
-                        first = 4 * (c * CHUNK_PATCHES + a)
-                        place = main_words[:, :, first : first + 4, :]
-                    if half == 0:
-                        nc.scalar.copy(out=place, in_=sorted_tokens)
-                    else:
-                        nc.vector.tensor_copy(out=place, in_=sorted_tokens)
-
-        quantised = {}
-        biased = {}
-        finished = {}
-
-        def quantise(g):
-            if g == TAIL:
-                tokens = tail_tokens[:].rearrange("q r a h v -> q (r a h v)")
-            else:
-                tiles = main_tokens[:, g * GROUP_TILES : (g + 1) * GROUP_TILES, :, :]
-                tokens = tiles.rearrange("q r p v -> q (r p v)")
-            codes = work.tile([P, GROUP_TOKENS], U32, align_bytes=64)
-            scales = work.tile([P, GROUP_TOKENS], U8, align_bytes=64)
-            nc.vector.quantize_mx(out=codes[:].bitcast(FP8X4), scales=scales[:], in_=tokens)
-            quantised[g] = (codes, scales)
-            biased[g] = work.tile([P, D_TILES, GROUP_TOKENS], F32, name="with_bias")
-            finished[g] = stores.tile([P, GROUP_TILES, D], F32, name="out_group")
-
-        def multiply(g, m):
-            codes, scales = quantised[g]
-            prod = psum_prod.tile([P, GROUP_TOKENS], F32, tag="prod")
-            multiply_by_w(prod[:], m, codes[:], scales[:])
-            nc.scalar.activation(
-                out=biased[g][:, m, :],
-                in_=prod[:],
-                func=IDENTITY,
-                bias=bias_col[:, m : m + 1],
-                scale=1.0,
+                    a = 2 * pair + i
+                    transpose_words(nc, flipped[:, i], ctx_chunks[c][:, a, :], by_row[:])
+                    nc.scalar.copy(
+                        out=grouped_words[:, :, a, :, :],
+                        in_=flipped[:, i].rearrange("q u (m h) -> q m h u", h=FRAME_GROUPS),
+                    )
+            codes = work.tile([P, RUN * P], U32, align_bytes=64)
+            scales = work.tile([P, RUN * P], U8, align_bytes=64)
+            nc.vector.quantize_mx(
+                out=codes[:].bitcast(FP8X4),
+                scales=scales[:],
+                in_=grouped[:].rearrange("q m a h v -> q (m a h v)"),
             )
-
-        def finish(g, i):
-            back = psum_back.tile([P, D], F32, tag="back")
-            for m in range(D_TILES):
-                nc.tensor.transpose(
-                    back[:, m * P : (m + 1) * P], biased[g][:, m, i * P : (i + 1) * P], ident[:]
+            out_chunk = resident.tile([P, RUN, D], F32, name="out_chunk%d" % c)
+            for j in range(RUN):
+                tokens = slice(j * P, (j + 1) * P)
+                prod = product(codes[:, tokens], scales[:, tokens])
+                nc.vector.tensor_tensor(
+                    out=out_chunk[:, j, :], in0=prod[:], in1=x_biased[:, j, :], op=ADD
                 )
-            nc.vector.tensor_tensor(
-                out=finished[g][:, i, :], in0=back[:], in1=x_groups[g][:, i, :], op=ADD
+            first_row = 1 + c * CHUNK_ROWS
+            nc.sync.dma_start(
+                out=out[:, first_row : first_row + CHUNK_ROWS, :].rearrange(
+                    "b (x j) d -> b x (j d)", j=RUN
+                ),
+                in_=out_chunk[:].rearrange("p j d -> p (j d)"),
             )
-
-        def store(g):
-            nc.sync.dma_start(out=rows_in_hbm(out, g), in_=rows_in_sbuf(finished[g], g))
-
-        flip_class()
-        flip(TAIL)
-        quantise(TAIL)
-        flip(0)
-        multiply_class()
-        flip(1)
-        for m in range(D_TILES):
-            multiply(TAIL, m)
-        flip(2)
-        finish_class()
-        for c in range(3, MAIN_CHUNKS):
-            flip(c)
-        quantise(group_order[1])
-        for k in range(1, len(group_order)):
-            if k + 1 < len(group_order):
-                quantise(group_order[k + 1])
-            for i in range(GROUP_TILES):
-                multiply(group_order[k], i)
-                finish(group_order[k - 1], i)
-            store(group_order[k - 1])
-        last = group_order[len(group_order) - 1]
-        for i in range(GROUP_TILES):
-            finish(last, i)
-        store(last)

@@ -9,6 +9,7 @@ U32 = mybir.dt.uint32
 U8 = mybir.dt.uint8
 FP8X4 = mybir.dt.float8_e4m3fn_x4
 ADD = mybir.AluOpType.add
+IDENTITY = mybir.ActivationFunctionType.Identity
 
 P = 128
 PACK = 4
@@ -16,14 +17,21 @@ SAMPLES = 16
 FRAMES = 8
 PATCHES = 36
 D = 512
+D_TILES = D // P
 
-RUN = 4
-CHUNK_ROWS = (P // SAMPLES) * RUN
-CHUNK_PATCHES = CHUNK_ROWS // FRAMES
+CHUNK_PATCHES = 4
 CHUNKS = PATCHES // CHUNK_PATCHES
-FRAME_GROUPS = FRAMES // RUN
+GROUP_TILES = 4
+GROUP_TOKENS = GROUP_TILES * P
 
-GPSIMD_TILES = 3
+MAIN_RUN = 2
+MAIN_ROWS = P * MAIN_RUN
+MAIN_CHUNKS = MAIN_ROWS // FRAMES // CHUNK_PATCHES
+GROUP_SAMPLES = GROUP_TILES // MAIN_RUN
+MAIN_GROUPS = SAMPLES // GROUP_SAMPLES
+TAIL_RUN = 4
+TAIL = MAIN_GROUPS
+TURN = 4
 
 FLOPS = 2 * SAMPLES * FRAMES * (1 + PATCHES) * D * D
 
@@ -34,17 +42,36 @@ def transpose_words(nc, flipped, rows, permutation):
         nc.tensor.transpose(flipped[:, u, :], words[:, u * P : (u + 1) * P], permutation)
 
 
+def rows_in_hbm(tensor, g):
+    if g == TAIL:
+        return tensor[:, 1 + MAIN_ROWS :, :].rearrange("b (x j) d -> b x (j d)", j=TAIL_RUN)
+    samples = tensor[g * GROUP_SAMPLES : (g + 1) * GROUP_SAMPLES, 1 : 1 + MAIN_ROWS, :]
+    return samples.rearrange("s (p j) d -> p s (j d)", j=MAIN_RUN)
+
+
+def rows_in_sbuf(tiles, g):
+    if g == TAIL:
+        return tiles[:].rearrange("p j d -> p (j d)")
+    return tiles[:].rearrange("p (s j) d -> p s (j d)", j=MAIN_RUN)
+
+
 def tile_timesformerlayer_pc_t_kernel(tc, ctx_s, x_res, s_out_w, s_out_b, out):
     nc = tc.nc
-    with ExitStack() as pools:
-        const = pools.enter_context(tc.tile_pool(name="const", bufs=1))
-        resident = pools.enter_context(tc.tile_pool(name="resident", bufs=1))
-        work = pools.enter_context(tc.tile_pool(name="work", bufs=3))
-        sums = pools.enter_context(tc.tile_pool(name="sums", bufs=4))
-        psum_bias = pools.enter_context(tc.psum_pool(name="psum_bias", bufs=1))
-        psum_flip = pools.enter_context(tc.psum_pool(name="psum_flip", bufs=3))
-        psum_prod = pools.enter_context(tc.psum_pool(name="psum_prod", bufs=4))
+    with ExitStack() as scope:
+        const = scope.enter_context(tc.tile_pool(name="const", bufs=1))
+        resident = scope.enter_context(tc.tile_pool(name="resident", bufs=1))
+        work = scope.enter_context(tc.tile_pool(name="work", bufs=3))
+        stores = scope.enter_context(tc.tile_pool(name="stores", bufs=4))
+        psum = scope.enter_context(tc.psum_pool(name="psum", bufs=8))
+        scope.enter_context(tc.manual_schedule())
 
+        group_order = [TAIL] + list(range(MAIN_GROUPS))
+
+        bias_rows = const.tile([P, P], BF16)
+        nc.vector.memset(bias_rows[:], 0.0)
+        nc.sync.dma_start(
+            out=bias_rows[0:D_TILES, :], in_=s_out_b.rearrange("(m d) -> m d", m=D_TILES)
+        )
         w_rows = const.tile([P, PACK, D], BF16)
         nc.sync.dma_start(
             out=w_rows[:].rearrange("q (u e) c -> q u (e c)", u=2),
@@ -52,54 +79,38 @@ def tile_timesformerlayer_pc_t_kernel(tc, ctx_s, x_res, s_out_w, s_out_b, out):
         )
         cls_ctx = resident.tile([P, D], BF16)
         nc.sync.dma_start(out=cls_ctx[:], in_=ctx_s[:, 0, :])
-        bias_row = const.tile([P, D], BF16)
-        nc.vector.memset(bias_row[:], 0.0)
-        nc.sync.dma_start(out=bias_row[0:1, :], in_=s_out_b.rearrange("(o d) -> o d", o=1))
         cls_x = resident.tile([SAMPLES, D], BF16)
         nc.sync.dma_start(out=cls_x[:], in_=x_res[:, 0, :])
-        ctx_chunks = []
-        x_chunks = []
-        for c in range(CHUNKS):
+        ctx_chunks = {}
+        for c in group_order:
             ctx_chunk = resident.tile([P, CHUNK_PATCHES, D], BF16, name="ctx_chunk%d" % c)
-            first_patch = 1 + c * CHUNK_PATCHES
-            nc.sync.dma_start(
-                out=ctx_chunk[:], in_=ctx_s[:, first_patch : first_patch + CHUNK_PATCHES, :]
-            )
-            ctx_chunks.append(ctx_chunk)
-            x_chunk = resident.tile([P, RUN, D], BF16, name="x_chunk%d" % c)
-            first_row = 1 + c * CHUNK_ROWS
-            nc.sync.dma_start(
-                out=x_chunk[:].rearrange("p j d -> p (j d)"),
-                in_=x_res[:, first_row : first_row + CHUNK_ROWS, :].rearrange(
-                    "b (x j) d -> b x (j d)", j=RUN
-                ),
-            )
-            x_chunks.append(x_chunk)
+            first = 1 + c * CHUNK_PATCHES
+            nc.sync.dma_start(out=ctx_chunk[:], in_=ctx_s[:, first : first + CHUNK_PATCHES, :])
+            ctx_chunks[c] = ctx_chunk
+        x_groups = {}
+        for g in group_order:
+            x_group = resident.tile([P, GROUP_TILES, D], BF16, name="x_group%d" % g)
+            nc.sync.dma_start(out=rows_in_sbuf(x_group, g), in_=rows_in_hbm(x_res, g))
+            x_groups[g] = x_group
 
         ident = const.tile([P, P], F32)
         make_identity(nc, ident[:])
-        by_row = const.tile([P, P], F32)
+        ident_bf16 = const.tile([P, P], BF16)
+        nc.vector.tensor_copy(out=ident_bf16[:], in_=ident[:])
+        main_order = const.tile([P, P], F32)
         nc.vector.tensor_copy(
-            out=by_row[:].rearrange("n (j g) -> n j g", j=RUN),
-            in_=ident[:].rearrange("n (g j) -> n j g", j=RUN),
+            out=main_order[:].rearrange("n (b j h) -> n b j h", j=MAIN_RUN, h=FRAMES // MAIN_RUN),
+            in_=ident[:].rearrange("n (b h j) -> n b j h", j=MAIN_RUN, h=FRAMES // MAIN_RUN),
         )
-        frame_mean = const.tile([P, P], F32)
-        nc.vector.memset(frame_mean[:], 0.0)
-        nc.vector.tensor_reduce(
-            out=frame_mean[:, 0:SAMPLES],
-            in_=ident[:].rearrange("n (b t) -> n b t", t=FRAMES),
-            axis=mybir.AxisListType.X,
-            op=ADD,
+        tail_order = const.tile([P, P], F32)
+        nc.vector.tensor_copy(
+            out=tail_order[:].rearrange("n (j g) -> n j g", j=TAIL_RUN),
+            in_=ident[:].rearrange("n (g j) -> n j g", j=TAIL_RUN),
         )
-        nc.vector.tensor_scalar_mul(
-            out=frame_mean[:, 0:SAMPLES], in0=frame_mean[:, 0:SAMPLES], scalar1=1.0 / FRAMES
-        )
-        ones = const.tile([P, P], BF16)
-        nc.vector.memset(ones[:], 1.0)
-        bias_psum = psum_bias.tile([P, D], F32)
-        nc.tensor.matmul(out=bias_psum[:], lhsT=ones[:], rhs=bias_row[:], start=True, stop=True)
-        bias_sbuf = const.tile([P, D], F32)
-        nc.scalar.copy(out=bias_sbuf[:], in_=bias_psum[:])
+        bias_flipped = psum.tile([P, P], BF16, tag="bank")
+        nc.tensor.transpose(bias_flipped[:], bias_rows[:], ident_bf16[:])
+        bias_col = const.tile([P, D_TILES], F32)
+        nc.scalar.copy(out=bias_col[:], in_=bias_flipped[:, 0:D_TILES])
 
         w_grouped = const.tile([P, D, PACK], BF16, align_bytes=64)
         nc.vector.tensor_copy(out=w_grouped[:], in_=w_rows[:].rearrange("q v c -> q c v"))
@@ -111,86 +122,165 @@ def tile_timesformerlayer_pc_t_kernel(tc, ctx_s, x_res, s_out_w, s_out_b, out):
             in_=w_grouped[:].rearrange("q c v -> q (c v)"),
         )
 
-        def product(codes, scales):
-            prod = psum_prod.tile([P, D], F32, tag="prod")
+        def multiply_by_w(prod, m, codes, scales):
+            columns = slice(m * P, (m + 1) * P)
             nc.tensor.matmul_mx(
-                out=prod[:],
-                lhsT=codes.bitcast(FP8X4),
-                lhsT_scale=scales,
-                rhs=w_codes[:].bitcast(FP8X4),
-                rhs_scale=w_scales[:],
+                out=prod,
+                lhsT=w_codes[:, columns].bitcast(FP8X4),
+                lhsT_scale=w_scales[:, columns],
+                rhs=codes.bitcast(FP8X4),
+                rhs_scale=scales,
                 start=True,
                 stop=True,
             )
-            return prod
 
-        cls_flipped = psum_flip.tile([P, 2, P], F32, tag="flipped")
-        transpose_words(nc, cls_flipped, cls_ctx[:], ident[:])
-        cls_grouped = const.tile([P, P, PACK], BF16, align_bytes=64)
-        nc.scalar.copy(
-            out=cls_grouped[:].bitcast(F32), in_=cls_flipped[:].rearrange("q u n -> q n u")
-        )
         cls_codes = const.tile([P, P], U32, align_bytes=64)
         cls_scales = const.tile([P, P], U8, align_bytes=64)
-        nc.vector.quantize_mx(
-            out=cls_codes[:].bitcast(FP8X4),
-            scales=cls_scales[:],
-            in_=cls_grouped[:].rearrange("q n v -> q (n v)"),
-        )
-        cls_prod = product(cls_codes[:], cls_scales[:])
-        cls_res = const.tile([P, D], F32)
-        nc.scalar.copy(out=cls_res[:], in_=cls_prod[:])
-        cls_mean = psum_prod.tile([P, D], F32, tag="prod")
-        nc.tensor.matmul(out=cls_mean[:], lhsT=frame_mean[:], rhs=cls_res[:], start=True, stop=True)
-        cls_out = const.tile([SAMPLES, D], F32)
-        nc.vector.tensor_tensor(out=cls_out[:], in0=cls_x[:], in1=bias_psum[0:SAMPLES, :], op=ADD)
-        nc.vector.tensor_tensor(out=cls_out[:], in0=cls_mean[0:SAMPLES, :], in1=cls_out[:], op=ADD)
-        nc.sync.dma_start(out=out[:, 0, :], in_=cls_out[:])
+        cls_mean = const.tile([P, D_TILES, P], F32)
+        nc.vector.memset(cls_mean[:], 0.0)
 
-        for c in range(CHUNKS):
-            x_biased = sums.tile([P, RUN, D], F32)
-            nc.gpsimd.tensor_tensor(
-                out=x_biased[:, 0:GPSIMD_TILES, :],
-                in0=x_chunks[c][:, 0:GPSIMD_TILES, :],
-                in1=bias_sbuf[:].unsqueeze(1).to_broadcast([P, GPSIMD_TILES, D]),
+        def flip_class():
+            cls_flipped = psum.tile([P, 2, P], F32, tag="bank")
+            transpose_words(nc, cls_flipped, cls_ctx[:], ident[:])
+            cls_grouped = const.tile([P, P, PACK], BF16, align_bytes=64)
+            nc.scalar.copy(
+                out=cls_grouped[:].bitcast(F32), in_=cls_flipped[:].rearrange("q u n -> q n u")
+            )
+            nc.vector.quantize_mx(
+                out=cls_codes[:].bitcast(FP8X4),
+                scales=cls_scales[:],
+                in_=cls_grouped[:].rearrange("q n v -> q (n v)"),
+            )
+
+        def multiply_class():
+            cls_prod = psum.tile([P, D_TILES, P], F32, tag="bank")
+            for m in range(D_TILES):
+                multiply_by_w(cls_prod[:, m, :], m, cls_codes[:], cls_scales[:])
+            cls_sum = const.tile([P, D_TILES, SAMPLES], F32)
+            nc.vector.tensor_reduce(
+                out=cls_sum[:],
+                in_=cls_prod[:].rearrange("i m (b t) -> i m b t", t=FRAMES),
+                axis=mybir.AxisListType.X,
                 op=ADD,
             )
-            for j in range(GPSIMD_TILES, RUN):
-                nc.vector.tensor_tensor(
-                    out=x_biased[:, j, :], in0=x_chunks[c][:, j, :], in1=bias_psum[:], op=ADD
+            for m in range(D_TILES):
+                nc.scalar.activation(
+                    out=cls_mean[:, m, 0:SAMPLES],
+                    in_=cls_sum[:, m, :],
+                    func=IDENTITY,
+                    bias=bias_col[:, m : m + 1],
+                    scale=1.0 / FRAMES,
                 )
 
-            grouped = work.tile(
-                [P, RUN * SAMPLES, CHUNK_PATCHES, FRAME_GROUPS, PACK], BF16, align_bytes=64
+        def finish_class():
+            cls_back = psum.tile([P, D], F32, tag="bank")
+            for m in range(D_TILES):
+                nc.tensor.transpose(cls_back[:, m * P : (m + 1) * P], cls_mean[:, m, :], ident[:])
+            cls_out = const.tile([SAMPLES, D], F32)
+            nc.vector.tensor_tensor(
+                out=cls_out[:], in0=cls_back[0:SAMPLES, :], in1=cls_x[:], op=ADD
             )
-            grouped_words = grouped[:].bitcast(F32)
-            for pair in range(CHUNK_PATCHES // 2):
-                flipped = psum_flip.tile([P, 2, 2, P], F32, tag="flipped")
+            nc.sync.dma_start(out=out[:, 0, :], in_=cls_out[:])
+
+        main_tokens = resident.tile([P, SAMPLES * MAIN_RUN, P, PACK], BF16, align_bytes=64)
+        main_words = main_tokens[:].bitcast(F32)
+        tail_tokens = resident.tile(
+            [P, TAIL_RUN * SAMPLES, CHUNK_PATCHES, FRAMES // TAIL_RUN, PACK], BF16, align_bytes=64
+        )
+        tail_words = tail_tokens[:].bitcast(F32)
+
+        def flip(c):
+            for half in range(2):
+                flipped = psum.tile([P, 2, 2, P], F32, tag="bank")
                 for i in range(2):
-                    a = 2 * pair + i
-                    transpose_words(nc, flipped[:, i], ctx_chunks[c][:, a, :], by_row[:])
-                    nc.scalar.copy(
-                        out=grouped_words[:, :, a, :, :],
-                        in_=flipped[:, i].rearrange("q u (m h) -> q m h u", h=FRAME_GROUPS),
-                    )
-            codes = work.tile([P, RUN * P], U32, align_bytes=64)
-            scales = work.tile([P, RUN * P], U8, align_bytes=64)
-            nc.vector.quantize_mx(
-                out=codes[:].bitcast(FP8X4),
-                scales=scales[:],
-                in_=grouped[:].rearrange("q m a h v -> q (m a h v)"),
+                    a = 2 * half + i
+                    order = tail_order if c == TAIL else main_order
+                    transpose_words(nc, flipped[:, i], ctx_chunks[c][:, a, :], order[:])
+                for i in range(2):
+                    a = 2 * half + i
+                    if c == TAIL:
+                        sorted_tokens = flipped[:, i].rearrange("q u (r h) -> q r h u", h=2)
+                        place = tail_words[:, :, a, :, :]
+                    else:
+                        sorted_tokens = flipped[:, i].rearrange("q u (r h) -> q r h u", h=4)
+                        first = 4 * (c * CHUNK_PATCHES + a)
+                        place = main_words[:, :, first : first + 4, :]
+                    if half == 0:
+                        nc.scalar.copy(out=place, in_=sorted_tokens)
+                    else:
+                        nc.vector.tensor_copy(out=place, in_=sorted_tokens)
+
+        quantised = {}
+        biased = {}
+        finished = {}
+
+        def quantise(g):
+            if g == TAIL:
+                tokens = tail_tokens[:].rearrange("q r a h v -> q (r a h v)")
+            else:
+                tiles = main_tokens[:, g * GROUP_TILES : (g + 1) * GROUP_TILES, :, :]
+                tokens = tiles.rearrange("q r p v -> q (r p v)")
+            codes = work.tile([P, GROUP_TOKENS], U32, align_bytes=64)
+            scales = work.tile([P, GROUP_TOKENS], U8, align_bytes=64)
+            nc.vector.quantize_mx(out=codes[:].bitcast(FP8X4), scales=scales[:], in_=tokens)
+            quantised[g] = (codes, scales)
+            biased[g] = work.tile([P, D_TILES, GROUP_TOKENS], F32, name="with_bias")
+            finished[g] = stores.tile([P, GROUP_TILES, D], F32, name="out_group")
+
+        def multiply(g, m):
+            codes, scales = quantised[g]
+            prod = psum.tile([P, GROUP_TOKENS], F32, tag="bank")
+            multiply_by_w(prod[:], m, codes[:], scales[:])
+            nc.scalar.activation(
+                out=biased[g][:, m, :],
+                in_=prod[:],
+                func=IDENTITY,
+                bias=bias_col[:, m : m + 1],
+                scale=1.0,
             )
-            out_chunk = resident.tile([P, RUN, D], F32, name="out_chunk%d" % c)
-            for j in range(RUN):
-                tokens = slice(j * P, (j + 1) * P)
-                prod = product(codes[:, tokens], scales[:, tokens])
-                nc.vector.tensor_tensor(
-                    out=out_chunk[:, j, :], in0=prod[:], in1=x_biased[:, j, :], op=ADD
+
+        def finish(g, i):
+            back = psum.tile([P, D], F32, tag="bank")
+            for m in range(D_TILES):
+                nc.tensor.transpose(
+                    back[:, m * P : (m + 1) * P], biased[g][:, m, i * P : (i + 1) * P], ident[:]
                 )
-            first_row = 1 + c * CHUNK_ROWS
-            nc.sync.dma_start(
-                out=out[:, first_row : first_row + CHUNK_ROWS, :].rearrange(
-                    "b (x j) d -> b x (j d)", j=RUN
-                ),
-                in_=out_chunk[:].rearrange("p j d -> p (j d)"),
+            nc.vector.tensor_tensor(
+                out=finished[g][:, i, :], in0=back[:], in1=x_groups[g][:, i, :], op=ADD
             )
+
+        def store(g):
+            if g == TAIL:
+                nc.sync.dma_start(out=rows_in_hbm(out, g), in_=rows_in_sbuf(finished[g], g))
+            else:
+                for s in range(GROUP_SAMPLES):
+                    nc.sync.dma_start(
+                        out=rows_in_hbm(out, g)[:, s, :], in_=rows_in_sbuf(finished[g], g)[:, s, :]
+                    )
+
+        flip_class()
+        flip(TAIL)
+        quantise(TAIL)
+        flip(0)
+        multiply_class()
+        flip(1)
+        for m in range(D_TILES):
+            multiply(TAIL, m)
+        flip(2)
+        finish_class()
+        for c in range(3, MAIN_CHUNKS):
+            flip(c)
+        quantise(group_order[1])
+        for k in range(1, len(group_order)):
+            if k + 1 < len(group_order):
+                quantise(group_order[k + 1])
+            for first in range(0, GROUP_TILES, TURN):
+                for i in range(first, first + TURN):
+                    multiply(group_order[k], i)
+                for i in range(first, first + TURN):
+                    finish(group_order[k - 1], i)
+            store(group_order[k - 1])
+        last = group_order[len(group_order) - 1]
+        for i in range(GROUP_TILES):
+            finish(last, i)
+        store(last)

@@ -31,7 +31,8 @@ GROUP_SAMPLES = GROUP_TILES // MAIN_RUN
 MAIN_GROUPS = SAMPLES // GROUP_SAMPLES
 TAIL_RUN = 4
 TAIL = MAIN_GROUPS
-TURN = 4
+
+GPSIMD_TILES = 1
 
 FLOPS = 2 * SAMPLES * FRAMES * (1 + PATCHES) * D * D
 
@@ -245,9 +246,16 @@ def tile_timesformerlayer_pc_t_kernel(tc, ctx_s, x_res, s_out_w, s_out_b, out):
                 nc.tensor.transpose(
                     back[:, m * P : (m + 1) * P], biased[g][:, m, i * P : (i + 1) * P], ident[:]
                 )
-            nc.vector.tensor_tensor(
-                out=finished[g][:, i, :], in0=back[:], in1=x_groups[g][:, i, :], op=ADD
-            )
+            if i < GPSIMD_TILES:
+                plain = work.tile([P, D], F32)
+                nc.scalar.copy(out=plain[:], in_=back[:])
+                nc.gpsimd.tensor_tensor(
+                    out=finished[g][:, i, :], in0=plain[:], in1=x_groups[g][:, i, :], op=ADD
+                )
+            else:
+                nc.vector.tensor_tensor(
+                    out=finished[g][:, i, :], in0=back[:], in1=x_groups[g][:, i, :], op=ADD
+                )
 
         def store(g):
             if g == TAIL:
@@ -258,29 +266,33 @@ def tile_timesformerlayer_pc_t_kernel(tc, ctx_s, x_res, s_out_w, s_out_b, out):
                         out=rows_in_hbm(out, g)[:, s, :], in_=rows_in_sbuf(finished[g], g)[:, s, :]
                     )
 
+        def multiply_group(g):
+            for m in range(D_TILES):
+                multiply(g, m)
+
+        def finish_group(g):
+            for i in range(GROUP_TILES):
+                finish(g, i)
+            store(g)
+
         flip_class()
         flip(TAIL)
         quantise(TAIL)
         flip(0)
         multiply_class()
         flip(1)
-        for m in range(D_TILES):
-            multiply(TAIL, m)
+        multiply_group(TAIL)
         flip(2)
         finish_class()
         for c in range(3, MAIN_CHUNKS):
             flip(c)
-        quantise(group_order[1])
-        for k in range(1, len(group_order)):
-            if k + 1 < len(group_order):
-                quantise(group_order[k + 1])
-            for first in range(0, GROUP_TILES, TURN):
-                for i in range(first, first + TURN):
-                    multiply(group_order[k], i)
-                for i in range(first, first + TURN):
-                    finish(group_order[k - 1], i)
-            store(group_order[k - 1])
-        last = group_order[len(group_order) - 1]
-        for i in range(GROUP_TILES):
-            finish(last, i)
-        store(last)
+        quantise(0)
+        finish_group(TAIL)
+        quantise(1)
+        multiply_group(0)
+        for g in range(1, MAIN_GROUPS):
+            if g + 1 < MAIN_GROUPS:
+                quantise(g + 1)
+            multiply_group(g)
+            finish_group(g - 1)
+        finish_group(MAIN_GROUPS - 1)

from contextlib import ExitStack

import concourse.mybir as mybir
from concourse.masks import make_identity

F32 = mybir.dt.float32
BF16 = mybir.dt.bfloat16
U32 = mybir.dt.uint32
U8 = mybir.dt.uint8
FP8X4 = mybir.dt.float8_e4m3fn_x4
ADD = mybir.AluOpType.add
IDENTITY = mybir.ActivationFunctionType.Identity

P = 128
PACK = 4
SAMPLES = 16
FRAMES = 8
PATCHES = 36
D = 512
D_TILES = D // P

CHUNK_PATCHES = 4
CHUNKS = PATCHES // CHUNK_PATCHES
GROUP_TILES = 4
GROUP_TOKENS = GROUP_TILES * P

MAIN_RUN = 2
MAIN_ROWS = P * MAIN_RUN
MAIN_CHUNKS = MAIN_ROWS // FRAMES // CHUNK_PATCHES
GROUP_SAMPLES = GROUP_TILES // MAIN_RUN
MAIN_GROUPS = SAMPLES // GROUP_SAMPLES
TAIL_RUN = 4
TAIL = MAIN_GROUPS

GPSIMD_TILES = 1

FLOPS = 2 * SAMPLES * FRAMES * (1 + PATCHES) * D * D


def transpose_words(nc, flipped, rows, permutation):
    words = rows.bitcast(F32)
    for u in range(2):
        nc.tensor.transpose(flipped[:, u, :], words[:, u * P : (u + 1) * P], permutation)


def rows_in_hbm(tensor, g):
    if g == TAIL:
        return tensor[:, 1 + MAIN_ROWS :, :].rearrange("b (x j) d -> b x (j d)", j=TAIL_RUN)
    samples = tensor[g * GROUP_SAMPLES : (g + 1) * GROUP_SAMPLES, 1 : 1 + MAIN_ROWS, :]
    return samples.rearrange("s (p j) d -> p s (j d)", j=MAIN_RUN)


def rows_in_sbuf(tiles, g):
    if g == TAIL:
        return tiles[:].rearrange("p j d -> p (j d)")
    return tiles[:].rearrange("p (s j) d -> p s (j d)", j=MAIN_RUN)


def tile_timesformerlayer_pc_t_kernel(tc, ctx_s, x_res, s_out_w, s_out_b, out):
    nc = tc.nc
    with ExitStack() as scope:
        const = scope.enter_context(tc.tile_pool(name="const", bufs=1))
        resident = scope.enter_context(tc.tile_pool(name="resident", bufs=1))
        work = scope.enter_context(tc.tile_pool(name="work", bufs=3))
        stores = scope.enter_context(tc.tile_pool(name="stores", bufs=4))
        psum = scope.enter_context(tc.psum_pool(name="psum", bufs=8))
        scope.enter_context(tc.manual_schedule())

        group_order = [TAIL] + list(range(MAIN_GROUPS))

        bias_rows = const.tile([P, P], BF16)
        nc.vector.memset(bias_rows[:], 0.0)
        nc.sync.dma_start(
            out=bias_rows[0:D_TILES, :], in_=s_out_b.rearrange("(m d) -> m d", m=D_TILES)
        )
        w_rows = const.tile([P, PACK, D], BF16)
        nc.sync.dma_start(
            out=w_rows[:].rearrange("q (u e) c -> q u (e c)", u=2),
            in_=s_out_w.rearrange("(u q e) c -> q u (e c)", u=2, e=2),
        )
        cls_ctx = resident.tile([P, D], BF16)
        nc.sync.dma_start(out=cls_ctx[:], in_=ctx_s[:, 0, :])
        cls_x = resident.tile([SAMPLES, D], BF16)
        nc.sync.dma_start(out=cls_x[:], in_=x_res[:, 0, :])
        ctx_chunks = {}
        for c in group_order:
            ctx_chunk = resident.tile([P, CHUNK_PATCHES, D], BF16, name="ctx_chunk%d" % c)
            first = 1 + c * CHUNK_PATCHES
            nc.sync.dma_start(out=ctx_chunk[:], in_=ctx_s[:, first : first + CHUNK_PATCHES, :])
            ctx_chunks[c] = ctx_chunk
        x_groups = {}
        for g in group_order:
            x_group = resident.tile([P, GROUP_TILES, D], BF16, name="x_group%d" % g)
            nc.sync.dma_start(out=rows_in_sbuf(x_group, g), in_=rows_in_hbm(x_res, g))
            x_groups[g] = x_group

        ident = const.tile([P, P], F32)
        make_identity(nc, ident[:])
        ident_bf16 = const.tile([P, P], BF16)
        nc.vector.tensor_copy(out=ident_bf16[:], in_=ident[:])
        main_order = const.tile([P, P], F32)
        nc.vector.tensor_copy(
            out=main_order[:].rearrange("n (b j h) -> n b j h", j=MAIN_RUN, h=FRAMES // MAIN_RUN),
            in_=ident[:].rearrange("n (b h j) -> n b j h", j=MAIN_RUN, h=FRAMES // MAIN_RUN),
        )
        tail_order = const.tile([P, P], F32)
        nc.vector.tensor_copy(
            out=tail_order[:].rearrange("n (j g) -> n j g", j=TAIL_RUN),
            in_=ident[:].rearrange("n (g j) -> n j g", j=TAIL_RUN),
        )
        bias_flipped = psum.tile([P, P], BF16, tag="bank")
        nc.tensor.transpose(bias_flipped[:], bias_rows[:], ident_bf16[:])
        bias_col = const.tile([P, D_TILES], F32)
        nc.scalar.copy(out=bias_col[:], in_=bias_flipped[:, 0:D_TILES])

        w_grouped = const.tile([P, D, PACK], BF16, align_bytes=64)
        nc.vector.tensor_copy(out=w_grouped[:], in_=w_rows[:].rearrange("q v c -> q c v"))
        w_codes = const.tile([P, D], U32, align_bytes=64)
        w_scales = const.tile([P, D], U8, align_bytes=64)
        nc.vector.quantize_mx(
            out=w_codes[:].bitcast(FP8X4),
            scales=w_scales[:],
            in_=w_grouped[:].rearrange("q c v -> q (c v)"),
        )

        def multiply_by_w(prod, m, codes, scales):
            columns = slice(m * P, (m + 1) * P)
            nc.tensor.matmul_mx(
                out=prod,
                lhsT=w_codes[:, columns].bitcast(FP8X4),
                lhsT_scale=w_scales[:, columns],
                rhs=codes.bitcast(FP8X4),
                rhs_scale=scales,
                start=True,
                stop=True,
            )

        cls_codes = const.tile([P, P], U32, align_bytes=64)
        cls_scales = const.tile([P, P], U8, align_bytes=64)
        cls_mean = const.tile([P, D_TILES, P], F32)
        nc.vector.memset(cls_mean[:], 0.0)

        def flip_class():
            cls_flipped = psum.tile([P, 2, P], F32, tag="bank")
            transpose_words(nc, cls_flipped, cls_ctx[:], ident[:])
            cls_grouped = const.tile([P, P, PACK], BF16, align_bytes=64)
            nc.scalar.copy(
                out=cls_grouped[:].bitcast(F32), in_=cls_flipped[:].rearrange("q u n -> q n u")
            )
            nc.vector.quantize_mx(
                out=cls_codes[:].bitcast(FP8X4),
                scales=cls_scales[:],
                in_=cls_grouped[:].rearrange("q n v -> q (n v)"),
            )

        def multiply_class():
            cls_prod = psum.tile([P, D_TILES, P], F32, tag="bank")
            for m in range(D_TILES):
                multiply_by_w(cls_prod[:, m, :], m, cls_codes[:], cls_scales[:])
            cls_sum = const.tile([P, D_TILES, SAMPLES], F32)
            nc.vector.tensor_reduce(
                out=cls_sum[:],
                in_=cls_prod[:].rearrange("i m (b t) -> i m b t", t=FRAMES),
                axis=mybir.AxisListType.X,
                op=ADD,
            )
            for m in range(D_TILES):
                nc.scalar.activation(
                    out=cls_mean[:, m, 0:SAMPLES],
                    in_=cls_sum[:, m, :],
                    func=IDENTITY,
                    bias=bias_col[:, m : m + 1],
                    scale=1.0 / FRAMES,
                )

        def finish_class():
            cls_back = psum.tile([P, D], F32, tag="bank")
            for m in range(D_TILES):
                nc.tensor.transpose(cls_back[:, m * P : (m + 1) * P], cls_mean[:, m, :], ident[:])
            cls_out = const.tile([SAMPLES, D], F32)
            nc.vector.tensor_tensor(
                out=cls_out[:], in0=cls_back[0:SAMPLES, :], in1=cls_x[:], op=ADD
            )
            nc.sync.dma_start(out=out[:, 0, :], in_=cls_out[:])

        main_tokens = resident.tile([P, SAMPLES * MAIN_RUN, P, PACK], BF16, align_bytes=64)
        main_words = main_tokens[:].bitcast(F32)
        tail_tokens = resident.tile(
            [P, TAIL_RUN * SAMPLES, CHUNK_PATCHES, FRAMES // TAIL_RUN, PACK], BF16, align_bytes=64
        )
        tail_words = tail_tokens[:].bitcast(F32)

        def flip(c):
            for half in range(2):
                flipped = psum.tile([P, 2, 2, P], F32, tag="bank")
                for i in range(2):
                    a = 2 * half + i
                    order = tail_order if c == TAIL else main_order
                    transpose_words(nc, flipped[:, i], ctx_chunks[c][:, a, :], order[:])
                for i in range(2):
                    a = 2 * half + i
                    if c == TAIL:
                        sorted_tokens = flipped[:, i].rearrange("q u (r h) -> q r h u", h=2)
                        place = tail_words[:, :, a, :, :]
                    else:
                        sorted_tokens = flipped[:, i].rearrange("q u (r h) -> q r h u", h=4)
                        first = 4 * (c * CHUNK_PATCHES + a)
                        place = main_words[:, :, first : first + 4, :]
                    if half == 0:
                        nc.scalar.copy(out=place, in_=sorted_tokens)
                    else:
                        nc.vector.tensor_copy(out=place, in_=sorted_tokens)

        quantised = {}
        biased = {}
        finished = {}

        def quantise(g):
            if g == TAIL:
                tokens = tail_tokens[:].rearrange("q r a h v -> q (r a h v)")
            else:
                tiles = main_tokens[:, g * GROUP_TILES : (g + 1) * GROUP_TILES, :, :]
                tokens = tiles.rearrange("q r p v -> q (r p v)")
            codes = work.tile([P, GROUP_TOKENS], U32, align_bytes=64)
            scales = work.tile([P, GROUP_TOKENS], U8, align_bytes=64)
            nc.vector.quantize_mx(out=codes[:].bitcast(FP8X4), scales=scales[:], in_=tokens)
            quantised[g] = (codes, scales)
            biased[g] = work.tile([P, D_TILES, GROUP_TOKENS], F32, name="with_bias")
            finished[g] = stores.tile([P, GROUP_TILES, D], F32, name="out_group")

        def multiply(g, m):
            codes, scales = quantised[g]
            prod = psum.tile([P, GROUP_TOKENS], F32, tag="bank")
            multiply_by_w(prod[:], m, codes[:], scales[:])
            nc.scalar.activation(
                out=biased[g][:, m, :],
                in_=prod[:],
                func=IDENTITY,
                bias=bias_col[:, m : m + 1],
                scale=1.0,
            )

        def finish(g, i):
            back = psum.tile([P, D], F32, tag="bank")
            for m in range(D_TILES):
                nc.tensor.transpose(
                    back[:, m * P : (m + 1) * P], biased[g][:, m, i * P : (i + 1) * P], ident[:]
                )
            if i < GPSIMD_TILES:
                plain = work.tile([P, D], F32)
                nc.scalar.copy(out=plain[:], in_=back[:])
                nc.gpsimd.tensor_tensor(
                    out=finished[g][:, i, :], in0=plain[:], in1=x_groups[g][:, i, :], op=ADD
                )
            else:
                nc.vector.tensor_tensor(
                    out=finished[g][:, i, :], in0=back[:], in1=x_groups[g][:, i, :], op=ADD
                )

        def store(g):
            if g == TAIL:
                nc.sync.dma_start(out=rows_in_hbm(out, g), in_=rows_in_sbuf(finished[g], g))
            else:
                for s in range(GROUP_SAMPLES):
                    nc.sync.dma_start(
                        out=rows_in_hbm(out, g)[:, s, :], in_=rows_in_sbuf(finished[g], g)[:, s, :]
                    )

        def multiply_group(g):
            for m in range(D_TILES):
                multiply(g, m)

        def finish_group(g):
            for i in range(GROUP_TILES):
                finish(g, i)
            store(g)

        flip_class()
        flip(TAIL)
        quantise(TAIL)
        flip(0)
        multiply_class()
        flip(1)
        multiply_group(TAIL)
        flip(2)
        finish_class()
        for c in range(3, MAIN_CHUNKS):
            flip(c)
        quantise(0)
        finish_group(TAIL)
        quantise(1)
        multiply_group(0)
        for g in range(1, MAIN_GROUPS):
            if g + 1 < MAIN_GROUPS:
                quantise(g + 1)
            multiply_group(g)
            finish_group(g - 1)
        finish_group(MAIN_GROUPS - 1)
